import numpy as np
import ml_dtypes


def mxq(x, axis, fmt="e4m3"):
    dtype, down = {"e4m3": (ml_dtypes.float8_e4m3fn, 7), "e5m2": (ml_dtypes.float8_e5m2, 14)}[fmt]
    v = np.moveaxis(np.asarray(x, np.float32).astype(ml_dtypes.bfloat16).astype(np.float64), axis, -1)
    blocks = v.reshape(v.shape[:-1] + (-1, 32))
    amax = np.abs(blocks).max(-1, keepdims=True)
    byte = np.maximum(np.where(amax > 0, np.frexp(amax)[1] - 1 + 127, 0) - down, 1)
    scale = np.exp2(byte - 127.0)
    codes = (blocks / scale).astype(np.float32).astype(dtype).astype(np.float64)
    return np.moveaxis((codes * scale).reshape(v.shape), -1, axis)


WIDE = False


def mx_kscale(k):
    if not WIDE:
        return np.ones(k)
    levels = np.array([10, -10, 5, -5, 0])
    if k % 512:
        return np.exp2(np.random.permutation(np.resize(levels, k // 32))).repeat(32)
    a = np.empty((k // 512, 16))
    for p in range(k // 512):
        a[p, :8] = np.random.permutation(np.resize(levels, 8))
        for g in range(8):
            far = levels[np.abs(levels - a[p, g]) >= 10]
            a[p, g + 8] = far[np.random.randint(len(far))]
    return np.exp2(a.ravel()).repeat(32)


BF16 = ml_dtypes.bfloat16


def bf(x):
    return np.asarray(x, np.float32).astype(BF16)


def f64(x):
    return np.asarray(x).astype(np.float64)


B, S, FIN, D, AF, F, H = 4, 1024, 128, 1024, 256, 4096, 16
MAX_TIMESCALE = 10000.0
MIN_TIMESCALE = 1.0
EPS = 1e-3


def timing_signal(length, channels):
    num_ts = channels // 2
    log_inc = np.log(MAX_TIMESCALE / MIN_TIMESCALE) / max(num_ts - 1, 1)
    inv_ts = MIN_TIMESCALE * np.exp(np.arange(num_ts) * -log_inc)
    scaled = np.arange(length)[:, None] * inv_ts[None, :]
    return np.concatenate([np.sin(scaled), np.cos(scaled)], axis=1)[None, :, :]


def layer_norm(v, gamma, beta):
    mu = v.mean(-1, keepdims=True)
    var = v.var(-1, keepdims=True)
    return (v - mu) / np.sqrt(var + EPS) * gamma + beta


def setup_inputs():
    r = np.random.standard_normal
    s = mx_kscale(D)
    return {"x": bf(r((B, S, FIN))),
            "W_emb": bf(r((FIN, D)) / np.sqrt(FIN)), "b_emb": bf(0.1 * r(D)),
            "g0": bf((1.0 + 0.1 * r(D)) * s), "beta0": bf(0.1 * r(D) * s),
            "Wq": bf(r((D, AF)) / np.sqrt(D) / s[:, None]), "bq": bf(0.1 * r(AF)),
            "Wk": bf(r((D, AF)) / np.sqrt(D) / s[:, None]), "bk": bf(0.1 * r(AF)),
            "Wv": bf(r((D, AF)) / np.sqrt(D) / s[:, None]), "bv": bf(0.1 * r(AF))}


def reference(x, W_emb, b_emb, g0, beta0, Wq, bq, Wk, bk, Wv, bv):
    h = np.maximum(f64(x) @ f64(W_emb) + f64(b_emb), 0.0)
    h = h + timing_signal(S, D)
    h = layer_norm(h, f64(g0), f64(beta0))
    hq = mxq(h, 2, "e4m3")
    q = (hq @ mxq(f64(Wq), 0, "e4m3")) + f64(bq)
    k = (hq @ mxq(f64(Wk), 0, "e4m3")) + f64(bk)
    v = (hq @ mxq(f64(Wv), 0, "e4m3")) + f64(bv)
    return q, k, v

@@ -1,0 +1,412 @@
+import math
+from contextlib import ExitStack
+
+import concourse.mybir as mybir
+from concourse.masks import make_identity
+
+F32 = mybir.dt.float32
+BF16 = mybir.dt.bfloat16
+I32 = mybir.dt.int32
+U32 = mybir.dt.uint32
+U8 = mybir.dt.uint8
+FP8X4 = mybir.dt.float8_e4m3fn_x4
+ALU = mybir.AluOpType
+FUNC = mybir.ActivationFunctionType
+
+P = 128
+BATCH = 4
+SEQ = 1024
+FIN = 128
+D = 1024
+N_OUT = 256
+N_ALL = 3 * N_OUT
+EPS = 1e-3
+BANK = 512
+HALVES = D // BANK
+PACK = 4
+K_PASS = P * PACK
+PASSES = D // K_PASS
+CHUNKS = D // P
+N_POS = SEQ // P
+GROUP = BATCH * P
+
+FLOPS = 2 * BATCH * SEQ * (FIN * D + D * N_ALL)
+
+N_FREQ = D // 2
+LOG_STEP = math.log(10000.0) / (N_FREQ - 1)
+FINE = 32
+COARSE = N_FREQ // FINE
+HEAD_BITS = 12
+ROUND_TO_INT = 12582912.0
+
+
+def head_of(value):
+    exponent = math.floor(math.log(value) / math.log(2.0))
+    step = 2.0 ** (exponent - HEAD_BITS + 1)
+    return round(value / step) * step
+
+
+def fill_table(nc, heads, tails, one, values):
+    for i, value in enumerate(values):
+        nc.vector.memset(heads[:, i : i + 1], head_of(value))
+        nc.scalar.mul(out=tails[:, i : i + 1], in_=one[:], mul=value - head_of(value))
+
+
+def tile_ffnn_encoder_pa_t_kernel(
+    tc, x, W_emb, b_emb, g0, beta0, Wq, bq, Wk, bk, Wv, bv, out_0, out_1, out_2
+):
+    nc = tc.nc
+    with ExitStack() as ctx:
+        ctx.enter_context(tc.manual_schedule())
+        keep = ctx.enter_context(tc.tile_pool(name="keep", bufs=1))
+        work = ctx.enter_context(tc.tile_pool(name="work", bufs=2))
+        psum_z = ctx.enter_context(tc.psum_pool(name="psum_z", bufs=2))
+        psum_t = ctx.enter_context(tc.psum_pool(name="psum_t", bufs=4))
+        psum_o = ctx.enter_context(tc.psum_pool(name="psum_o", bufs=1))
+
+        x_by_pos = x.rearrange("b (a p) f -> a p b f", p=P)
+        x_sb = keep.tile([P, N_POS, BATCH, FIN], BF16)
+        nc.sync.dma_start(out=x_sb[:, 0], in_=x_by_pos[0])
+        w_emb_raw = keep.tile([P, D], BF16)
+        nc.sync.dma_start(out=w_emb_raw[:], in_=W_emb)
+        vectors = keep.tile([P, 3, 2 * CHUNKS], BF16)
+        for v, vector in enumerate((b_emb, g0, beta0)):
+            nc.sync.dma_start(
+                out=vectors[:, v, 0:CHUNKS].rearrange("p (g t) -> p g t", t=PACK),
+                in_=vector.rearrange("(g p t) -> p g t", p=P, t=PACK),
+            )
+        for a in range(1, N_POS):
+            nc.sync.dma_start(out=x_sb[:, a], in_=x_by_pos[a])
+        w_raw = []
+        for w, weight in enumerate((Wq, Wk, Wv)):
+            raw = keep.tile([P, PASSES, PACK, N_OUT], BF16, name="w_raw%d" % w)
+            nc.sync.dma_start(
+                out=raw[:], in_=weight.rearrange("(g p t) n -> p g t n", p=P, t=PACK)
+            )
+            w_raw.append(raw)
+        bias_qkv = keep.tile([P, N_ALL], BF16)
+        for w, vector in enumerate((bq, bk, bv)):
+            nc.sync.dma_start(
+                out=bias_qkv[:, w * N_OUT : (w + 1) * N_OUT], in_=vector.partition_broadcast(P)
+            )
+
+        ident_b = keep.tile([P, P], BF16)
+        make_identity(nc, ident_b[:])
+        ident_f = keep.tile([P, P], F32)
+        make_identity(nc, ident_f[:])
+        pos_i = keep.tile([P, N_POS], I32)
+        nc.gpsimd.iota(out=pos_i[:], pattern=[[P, N_POS]], base=0, channel_multiplier=1)
+        one = keep.tile([P, 1], F32)
+        nc.vector.memset(one[:], 1.0)
+        minus_eighth = keep.tile([P, 1], F32)
+        nc.vector.memset(minus_eighth[:], -0.125)
+        plus_eighth = keep.tile([P, 1], F32)
+        nc.vector.memset(plus_eighth[:], 0.125)
+        minus_half = keep.tile([P, BATCH], F32)
+        nc.vector.memset(minus_half[:], -0.5)
+        quarter_turn = keep.tile([P, 1], F32)
+        nc.scalar.mul(out=quarter_turn[:], in_=one[:], mul=0.5 * math.pi)
+
+        coarse_hd = keep.tile([P, COARSE], F32)
+        coarse_tl = keep.tile([P, COARSE], F32)
+        fill_table(
+            nc, coarse_hd, coarse_tl, one,
+            [math.exp(-FINE * i * LOG_STEP) / (2.0 * math.pi) for i in range(COARSE)],
+        )
+        fine_hd = keep.tile([P, FINE], F32)
+        fine_tl = keep.tile([P, FINE], F32)
+        fill_table(nc, fine_hd, fine_tl, one, [math.exp(-i * LOG_STEP) for i in range(FINE)])
+
+        QUADS = FINE // PACK
+
+        def over_fine(table):
+            return table[:].unsqueeze(2).unsqueeze(3).to_broadcast([P, COARSE, QUADS, PACK])
+
+        def over_coarse(table):
+            quads = table[:].rearrange("p (q t) -> p q t", t=PACK)
+            return quads.unsqueeze(1).to_broadcast([P, COARSE, QUADS, PACK])
+
+        def as_grid(flat):
+            return flat[:].rearrange("p (t a q) -> p a q t", t=PACK, q=QUADS)
+
+        product = keep.tile([P, N_FREQ], F32)
+        cross = keep.tile([P, N_FREQ], F32)
+        cross2 = keep.tile([P, N_FREQ], F32)
+        f_head = keep.tile([P, N_FREQ], F32)
+        f_tail = keep.tile([P, N_FREQ], F32)
+        nc.vector.tensor_tensor(
+            out=as_grid(product), in0=over_fine(coarse_hd), in1=over_coarse(fine_hd), op=ALU.mult
+        )
+        nc.vector.tensor_single_scalar(
+            out=f_head[:].bitcast(I32), in_=product[:].bitcast(I32), scalar=-2048, op=ALU.bitwise_and
+        )
+        pos = keep.tile([P, N_POS], F32)
+        nc.vector.tensor_copy(out=pos[:], in_=pos_i[:])
+        fine_all = keep.tile([P, FINE], F32)
+        nc.vector.tensor_tensor(out=fine_all[:], in0=fine_hd[:], in1=fine_tl[:], op=ALU.add)
+        nc.vector.tensor_tensor(
+            out=as_grid(cross), in0=over_fine(coarse_hd), in1=over_coarse(fine_tl), op=ALU.mult
+        )
+        nc.vector.tensor_tensor(
+            out=as_grid(cross2), in0=over_fine(coarse_tl), in1=over_coarse(fine_all), op=ALU.mult
+        )
+        nc.vector.tensor_tensor(out=cross[:], in0=cross[:], in1=cross2[:], op=ALU.add)
+        nc.vector.tensor_tensor(out=product[:], in0=product[:], in1=f_head[:], op=ALU.subtract)
+        nc.vector.tensor_tensor(out=f_tail[:], in0=product[:], in1=cross[:], op=ALU.add)
+
+        cols = keep.tile([P, 3 * CHUNKS], F32)
+        nc.vector.tensor_copy(
+            out=cols[:].rearrange("p (v c) -> p v c", v=3), in_=vectors[:, :, 0:CHUNKS]
+        )
+        b_wide = keep.tile([P, CHUNKS, P], F32)
+        nc.vector.tensor_copy(
+            out=b_wide[:], in_=cols[:, 0:CHUNKS].unsqueeze(2).to_broadcast([P, CHUNKS, P])
+        )
+
+        w_emb = keep.tile([P, D], BF16)
+        nc.scalar.copy(
+            out=w_emb[:].rearrange("f (g t p) -> f g t p", g=PASSES, t=PACK),
+            in_=w_emb_raw[:].rearrange("f (g p t) -> f g t p", g=PASSES, t=PACK),
+        )
+
+        w_codes = keep.tile([P, PASSES, N_ALL], U32, align_bytes=64)
+        w_scales = keep.tile([P, PASSES, N_ALL], U8, align_bytes=64)
+
+        def regroup_weight(w):
+            w_grouped = work.tile([P, PASSES, N_OUT, PACK], BF16, bufs=2, align_bytes=64)
+            nc.scalar.copy(out=w_grouped[:], in_=w_raw[w][:].rearrange("p g t n -> p g n t"))
+            return w_grouped
+
+        def quantise_weight(w, w_grouped):
+            for g in range(PASSES):
+                cols_w = slice(w * N_OUT, (w + 1) * N_OUT)
+                nc.vector.quantize_mx(
+                    out=w_codes[:, g, cols_w].bitcast(FP8X4),
+                    scales=w_scales[:, g, cols_w],
+                    in_=w_grouped[:, g].rearrange("p n t -> p (n t)"),
+                )
+
+        timing = keep.tile([P, N_POS, D], F32)
+
+        def make_timing(a):
+            here = pos[:, a : a + 1]
+            turns = work.tile([P, N_FREQ], F32, bufs=2)
+            nc.vector.tensor_scalar(
+                out=turns[:], in0=f_head[:], scalar1=here, scalar2=-0.125, op0=ALU.mult, op1=ALU.add
+            )
+            whole = work.tile([P, N_FREQ], F32, bufs=2)
+            nc.vector.tensor_scalar(
+                out=whole[:], in0=turns[:], scalar1=ROUND_TO_INT, scalar2=ROUND_TO_INT,
+                op0=ALU.add, op1=ALU.subtract,
+            )
+            nc.vector.tensor_tensor(out=whole[:], in0=turns[:], in1=whole[:], op=ALU.subtract)
+            frac = work.tile([P, N_FREQ], F32, bufs=2)
+            nc.vector.scalar_tensor_tensor(
+                out=frac[:], in0=f_tail[:], scalar=here, in1=whole[:], op0=ALU.mult, op1=ALU.add
+            )
+            distance = work.tile([P, D], F32, bufs=2)
+            nc.scalar.activation(
+                out=distance[:, 0:N_FREQ], in_=frac[:], func=FUNC.Abs, bias=minus_eighth[:], scale=1.0
+            )
+            nc.scalar.activation(
+                out=distance[:, N_FREQ:D], in_=frac[:], func=FUNC.Abs, bias=plus_eighth[:], scale=1.0
+            )
+            nc.scalar.activation(
+                out=timing[:, a, :], in_=distance[:], func=FUNC.Sin,
+                bias=quarter_turn[:], scale=-2.0 * math.pi,
+            )
+
+        def transpose_x(a):
+            x_t_ps = psum_t.tile([P, GROUP], BF16, tag="tp")
+            for b in range(BATCH):
+                nc.tensor.transpose(
+                    out=x_t_ps[:, b * P : (b + 1) * P], in_=x_sb[:, a, b, :], identity=ident_b[:]
+                )
+            x_t = work.tile([P, GROUP], BF16, bufs=2)
+            nc.scalar.copy(out=x_t[:], in_=x_t_ps[:])
+            return x_t
+
+        def embed_bank(a, b, half, x_t, e, sum_e):
+            z = psum_z.tile([P, BANK], F32)
+            for j in range(BANK // P):
+                nc.tensor.matmul(
+                    out=z[:, j * P : (j + 1) * P],
+                    lhsT=b_wide[:, half * (BANK // P) + j, :],
+                    rhs=ident_f[:],
+                    is_transpose=True,
+                    start=(j == 0),
+                    stop=False,
+                )
+            nc.tensor.matmul(
+                out=z[:],
+                lhsT=x_t[:, b * P : (b + 1) * P],
+                rhs=w_emb[:, half * BANK : (half + 1) * BANK],
+                start=False,
+                stop=True,
+            )
+            nc.vector.scalar_tensor_tensor(
+                out=e[:, half * BANK : (half + 1) * BANK],
+                in0=z[:],
+                scalar=0.0,
+                in1=timing[:, a, half * BANK : (half + 1) * BANK],
+                op0=ALU.max,
+                op1=ALU.add,
+                accum_out=sum_e[:, b, half : half + 1],
+            )
+
+        def sum_of_squares(e, b, sum_sq):
+            squares = work.tile([P, D], BF16, bufs=2)
+            nc.scalar.activation(
+                out=squares[:], in_=e[:], func=FUNC.Square, accum_out=sum_sq[:, b : b + 1]
+            )
+
+        def normalise(e_tiles, sum_e, sum_sq):
+            total = work.tile([P, BATCH], F32, bufs=2)
+            nc.gpsimd.tensor_tensor(out=total[:], in0=sum_e[:, :, 0], in1=sum_e[:, :, 1], op=ALU.add)
+            minus_mean = work.tile([P, BATCH], F32, bufs=2)
+            nc.gpsimd.tensor_scalar(
+                out=minus_mean[:], in0=total[:], scalar1=-1.0 / D, scalar2=0.0, op0=ALU.mult, op1=ALU.add
+            )
+            mean_sq = work.tile([P, BATCH], F32, bufs=2)
+            nc.gpsimd.tensor_tensor(out=mean_sq[:], in0=minus_mean[:], in1=minus_mean[:], op=ALU.mult)
+            var_eps = work.tile([P, BATCH], F32, bufs=2)
+            nc.gpsimd.tensor_scalar(
+                out=var_eps[:], in0=sum_sq[:], scalar1=1.0 / D, scalar2=EPS, op0=ALU.mult, op1=ALU.add
+            )
+            nc.gpsimd.tensor_tensor(out=var_eps[:], in0=var_eps[:], in1=mean_sq[:], op=ALU.subtract)
+            rstd = work.tile([P, BATCH], F32, bufs=2)
+            nc.gpsimd.tensor_tensor(out=rstd[:], in0=var_eps[:], in1=minus_half[:], op=ALU.pow)
+            shift = work.tile([P, BATCH], F32, bufs=2)
+            nc.gpsimd.tensor_tensor(out=shift[:], in0=minus_mean[:], in1=rstd[:], op=ALU.mult)
+            normed_tiles = []
+            for b in range(BATCH):
+                normed = work.tile([P, D], F32, name="normed%d" % b, tag="normed", bufs=8)
+                nc.gpsimd.tensor_scalar(
+                    out=normed[:], in0=e_tiles[b][:], scalar1=rstd[:, b : b + 1],
+                    scalar2=shift[:, b : b + 1], op0=ALU.mult, op1=ALU.add,
+                )
+                normed_tiles.append(normed)
+            return normed_tiles
+
+        def scale_and_shift(normed_tiles, c, planes):
+            normed_t = psum_t.tile([P, GROUP], F32, tag="tp")
+            for b in range(BATCH):
+                nc.tensor.transpose(
+                    out=normed_t[:, b * P : (b + 1) * P],
+                    in_=normed_tiles[b][:, c * P : (c + 1) * P],
+                    identity=ident_f[:],
+                )
+            nc.scalar.activation(
+                out=planes[:, c % PACK, :], in_=normed_t[:], func=FUNC.Identity,
+                scale=cols[:, CHUNKS + c : CHUNKS + c + 1],
+                bias=cols[:, 2 * CHUNKS + c : 2 * CHUNKS + c + 1],
+            )
+
+        def regroup(planes):
+            grouped = work.tile([P, GROUP, PACK], BF16, bufs=2, align_bytes=64)
+            nc.vector.tensor_copy(out=grouped[:], in_=planes[:].rearrange("p t r -> p r t"))
+            return grouped
+
+        def quantise(grouped):
+            codes = work.tile([P, GROUP], U32, bufs=4, align_bytes=64)
+            scales = work.tile([P, GROUP], U8, bufs=4, align_bytes=64)
+            nc.vector.quantize_mx(
+                out=codes[:].bitcast(FP8X4),
+                scales=scales[:],
+                in_=grouped[:].rearrange("p r t -> p (r t)"),
+            )
+            return codes, scales
+
+        def project(b, h_mx, result):
+            tokens = slice(b * P, (b + 1) * P)
+            for name, first, width in (("acc_qk", 0, BANK), ("acc_v", BANK, N_ALL - BANK)):
+                acc = psum_o.tile([P, width], F32, name=name, tag=name)
+                for g in range(PASSES):
+                    codes, scales = h_mx[g]
+                    nc.tensor.matmul_mx(
+                        out=acc[:],
+                        lhsT=codes[:, tokens].bitcast(FP8X4),
+                        lhsT_scale=scales[:, tokens],
+                        rhs=w_codes[:, g, first : first + width].bitcast(FP8X4),
+                        rhs_scale=w_scales[:, g, first : first + width],
+                        start=(g == 0),
+                        stop=(g == PASSES - 1),
+                    )
+                nc.vector.tensor_tensor(
+                    out=result[:, b, first : first + width], in0=acc[:],
+                    in1=bias_qkv[:, first : first + width], op=ALU.add,
+                )
+
+        NORM_AT = BATCH
+        CHUNKS_AT = 2 * BATCH
+        PROJECT_AT = 3 * BATCH + 1
+        CHUNKS_A_STEP = CHUNKS // BATCH
+
+        def group_at(step, lag):
+            group, place = divmod(step - lag, BATCH)
+            return (group if 0 <= group < N_POS else None), place
+
+        x_t_of = {0: transpose_x(0)}
+        make_timing(0)
+        sums_of = {}
+        e_of = {}
+        normed_of = {}
+        h_mx_of = {}
+        w_grouped_of = {}
+        waiting = None
+        for step in range(BATCH * N_POS + PROJECT_AT):
+            group, b = group_at(step, 0)
+            if group is not None:
+                if b == 0:
+                    sum_e = work.tile([P, BATCH, HALVES], F32, bufs=3)
+                    sum_sq = work.tile([P, BATCH], F32, bufs=3)
+                    sums_of[group] = (sum_e, sum_sq)
+                    e_of[group] = []
+                e = work.tile([P, D], F32, bufs=8)
+                e_of[group].append(e)
+                for half in range(HALVES):
+                    embed_bank(group, b, half, x_t_of[group], e, sums_of[group][0])
+            if step + 1 < N_POS:
+                make_timing(step + 1)
+
+            done, place = group_at(step, NORM_AT)
+            if done is not None and place == 0:
+                normed_of[done] = normalise(e_of[done], sums_of[done][0], sums_of[done][1])
+            if group is not None and b == 1 and 1 <= group <= 3:
+                quantise_weight(group - 1, w_grouped_of[group - 1])
+
+            grouped = None
+            if waiting is not None:
+                grouped = regroup(waiting[1])
+            turned, j = group_at(step, CHUNKS_AT)
+            if turned is not None:
+                for c in range(j * CHUNKS_A_STEP, (j + 1) * CHUNKS_A_STEP):
+                    if c == 0:
+                        h_mx_of[turned] = []
+                    if c % PACK == 0:
+                        planes = work.tile([P, PACK, GROUP], BF16, bufs=2)
+                    scale_and_shift(normed_of[turned], c, planes)
+
+            if group is not None:
+                sum_of_squares(e, b, sums_of[group][1])
+                if b == 2 and group + 1 < N_POS:
+                    x_t_of[group + 1] = transpose_x(group + 1)
+                if b == 3 and group < 3:
+                    w_grouped_of[group] = regroup_weight(group)
+
+            ready, tile_b = group_at(step, PROJECT_AT)
+            if ready is not None:
+                if tile_b == 0:
+                    result = work.tile([P, BATCH, N_ALL], F32, bufs=2)
+                project(tile_b, h_mx_of[ready], result)
+                if tile_b == BATCH - 1:
+                    for w, out in enumerate((out_0, out_1, out_2)):
+                        nc.sync.dma_start(
+                            out=out.rearrange("b (a p) n -> a p b n", p=P)[ready],
+                            in_=result[:, :, w * N_OUT : (w + 1) * N_OUT],
+                        )
+            if grouped is not None:
+                h_mx_of[waiting[0]].append(quantise(grouped))
+                waiting = None
+            if turned is not None and (j + 1) * CHUNKS_A_STEP % PACK == 0:
+                waiting = (turned, planes)

@@ -36,6 +36,7 @@ N_FREQ = D // 2
 LOG_STEP = math.log(10000.0) / (N_FREQ - 1)
 FINE = 32
 COARSE = N_FREQ // FINE
+QUADS = FINE // PACK
 HEAD_BITS = 12
 ROUND_TO_INT = 12582912.0
 
@@ -46,10 +47,13 @@ def head_of(value):
     return round(value / step) * step
 
 
-def fill_table(nc, heads, tails, one, values):
-    for i, value in enumerate(values):
-        nc.vector.memset(heads[:, i : i + 1], head_of(value))
-        nc.scalar.mul(out=tails[:, i : i + 1], in_=one[:], mul=value - head_of(value))
+def fast_quads(a):
+    last = P * a + P - 1
+    return math.ceil(math.log(last / math.pi) / LOG_STEP / PACK)
+
+
+FAST_COARSE = math.ceil(fast_quads(N_POS - 1) / QUADS)
+SLOW_FROM = fast_quads(0) // QUADS
 
 
 def tile_ffnn_encoder_pa_t_kernel(
@@ -61,20 +65,23 @@ def tile_ffnn_encoder_pa_t_kernel(
         keep = ctx.enter_context(tc.tile_pool(name="keep", bufs=1))
         work = ctx.enter_context(tc.tile_pool(name="work", bufs=2))
         psum_z = ctx.enter_context(tc.psum_pool(name="psum_z", bufs=2))
-        psum_t = ctx.enter_context(tc.psum_pool(name="psum_t", bufs=4))
-        psum_o = ctx.enter_context(tc.psum_pool(name="psum_o", bufs=1))
+        psum_t = ctx.enter_context(tc.psum_pool(name="psum_t", bufs=3))
+        psum_o = ctx.enter_context(tc.psum_pool(name="psum_o", bufs=2))
 
         x_by_pos = x.rearrange("b (a p) f -> a p b f", p=P)
         x_sb = keep.tile([P, N_POS, BATCH, FIN], BF16)
         nc.sync.dma_start(out=x_sb[:, 0], in_=x_by_pos[0])
-        w_emb_raw = keep.tile([P, D], BF16)
-        nc.sync.dma_start(out=w_emb_raw[:], in_=W_emb)
         vectors = keep.tile([P, 3, 2 * CHUNKS], BF16)
-        for v, vector in enumerate((b_emb, g0, beta0)):
+
+        def load_vector(v, vector):
             nc.sync.dma_start(
                 out=vectors[:, v, 0:CHUNKS].rearrange("p (g t) -> p g t", t=PACK),
                 in_=vector.rearrange("(g p t) -> p g t", p=P, t=PACK),
             )
+
+        load_vector(0, b_emb)
+        w_emb_raw = keep.tile([P, D], BF16)
+        nc.sync.dma_start(out=w_emb_raw[:], in_=W_emb)
         for a in range(1, N_POS):
             nc.sync.dma_start(out=x_sb[:, a], in_=x_by_pos[a])
         w_raw = []
@@ -84,97 +91,124 @@ def tile_ffnn_encoder_pa_t_kernel(
                 out=raw[:], in_=weight.rearrange("(g p t) n -> p g t n", p=P, t=PACK)
             )
             w_raw.append(raw)
+        load_vector(1, g0)
+        load_vector(2, beta0)
         bias_qkv = keep.tile([P, N_ALL], BF16)
         for w, vector in enumerate((bq, bk, bv)):
             nc.sync.dma_start(
                 out=bias_qkv[:, w * N_OUT : (w + 1) * N_OUT], in_=vector.partition_broadcast(P)
             )
 
-        ident_b = keep.tile([P, P], BF16)
-        make_identity(nc, ident_b[:])
-        ident_f = keep.tile([P, P], F32)
-        make_identity(nc, ident_f[:])
-        pos_i = keep.tile([P, N_POS], I32)
-        nc.gpsimd.iota(out=pos_i[:], pattern=[[P, N_POS]], base=0, channel_multiplier=1)
         one = keep.tile([P, 1], F32)
         nc.vector.memset(one[:], 1.0)
+        warm = keep.tile([P, 1], F32)
+        nc.scalar.activation(out=warm[:], in_=one[:], func=FUNC.Sin)
+        ident_b = keep.tile([P, P], BF16)
+        make_identity(nc, ident_b[:])
+        coarse_hd = keep.tile([P, COARSE], F32)
+        coarse_tl = keep.tile([P, COARSE], F32)
+        fine_hd = keep.tile([P, FINE], F32)
+        fine_tl = keep.tile([P, FINE], F32)
+        coarse_values = [math.exp(-FINE * i * LOG_STEP) / (2.0 * math.pi) for i in range(COARSE)]
+        fine_values = [math.exp(-i * LOG_STEP) for i in range(FINE)]
+        for i, value in enumerate(coarse_values):
+            nc.vector.memset(coarse_hd[:, i : i + 1], head_of(value))
+            nc.scalar.mul(out=coarse_tl[:, i : i + 1], in_=one[:], mul=value - head_of(value))
+        for i, value in enumerate(fine_values):
+            nc.gpsimd.memset(fine_hd[:, i : i + 1], head_of(value))
+            nc.vector.tensor_scalar_mul(fine_tl[:, i : i + 1], one[:], value - head_of(value))
+        ident_f = keep.tile([P, P], F32)
+        make_identity(nc, ident_f[:])
         minus_eighth = keep.tile([P, 1], F32)
-        nc.vector.memset(minus_eighth[:], -0.125)
+        nc.gpsimd.memset(minus_eighth[:], -0.125)
         plus_eighth = keep.tile([P, 1], F32)
-        nc.vector.memset(plus_eighth[:], 0.125)
+        nc.gpsimd.memset(plus_eighth[:], 0.125)
         minus_half = keep.tile([P, BATCH], F32)
-        nc.vector.memset(minus_half[:], -0.5)
+        nc.gpsimd.memset(minus_half[:], -0.5)
+        pos = keep.tile([P, N_POS], F32)
+        nc.gpsimd.iota(
+            out=pos[:], pattern=[[P, N_POS]], base=0, channel_multiplier=1,
+            allow_small_or_imprecise_dtypes=True,
+        )
         quarter_turn = keep.tile([P, 1], F32)
         nc.scalar.mul(out=quarter_turn[:], in_=one[:], mul=0.5 * math.pi)
 
-        coarse_hd = keep.tile([P, COARSE], F32)
-        coarse_tl = keep.tile([P, COARSE], F32)
-        fill_table(
-            nc, coarse_hd, coarse_tl, one,
-            [math.exp(-FINE * i * LOG_STEP) / (2.0 * math.pi) for i in range(COARSE)],
-        )
-        fine_hd = keep.tile([P, FINE], F32)
-        fine_tl = keep.tile([P, FINE], F32)
-        fill_table(nc, fine_hd, fine_tl, one, [math.exp(-i * LOG_STEP) for i in range(FINE)])
+        def over_fine(table, first, last):
+            cells = table[:, first:last].unsqueeze(2).unsqueeze(3)
+            return cells.to_broadcast([P, last - first, QUADS, PACK])
 
-        QUADS = FINE // PACK
-
-        def over_fine(table):
-            return table[:].unsqueeze(2).unsqueeze(3).to_broadcast([P, COARSE, QUADS, PACK])
-
-        def over_coarse(table):
+        def over_coarse(table, count):
             quads = table[:].rearrange("p (q t) -> p q t", t=PACK)
-            return quads.unsqueeze(1).to_broadcast([P, COARSE, QUADS, PACK])
+            return quads.unsqueeze(1).to_broadcast([P, count, QUADS, PACK])
 
-        def as_grid(flat):
-            return flat[:].rearrange("p (t a q) -> p a q t", t=PACK, q=QUADS)
+        def as_grid(table):
+            return table[:].rearrange("p t (a q) -> p a q t", q=QUADS)
 
-        product = keep.tile([P, N_FREQ], F32)
-        cross = keep.tile([P, N_FREQ], F32)
-        cross2 = keep.tile([P, N_FREQ], F32)
-        f_head = keep.tile([P, N_FREQ], F32)
-        f_tail = keep.tile([P, N_FREQ], F32)
+        fast_shape = [P, PACK, FAST_COARSE * QUADS]
+        product = keep.tile(fast_shape, F32)
+        cross = keep.tile(fast_shape, F32)
+        cross2 = keep.tile(fast_shape, F32)
+        f_head = keep.tile(fast_shape, F32)
+        f_tail = keep.tile(fast_shape, F32)
+        f_slow = keep.tile([P, PACK, (COARSE - SLOW_FROM) * QUADS], F32)
+        fine_all = keep.tile([P, FINE], F32)
+        coarse_all = keep.tile([P, COARSE], F32)
         nc.vector.tensor_tensor(
-            out=as_grid(product), in0=over_fine(coarse_hd), in1=over_coarse(fine_hd), op=ALU.mult
+            out=as_grid(product), in0=over_fine(coarse_hd, 0, FAST_COARSE),
+            in1=over_coarse(fine_hd, FAST_COARSE), op=ALU.mult,
         )
         nc.vector.tensor_single_scalar(
             out=f_head[:].bitcast(I32), in_=product[:].bitcast(I32), scalar=-2048, op=ALU.bitwise_and
         )
-        pos = keep.tile([P, N_POS], F32)
-        nc.vector.tensor_copy(out=pos[:], in_=pos_i[:])
-        fine_all = keep.tile([P, FINE], F32)
-        nc.vector.tensor_tensor(out=fine_all[:], in0=fine_hd[:], in1=fine_tl[:], op=ALU.add)
-        nc.vector.tensor_tensor(
-            out=as_grid(cross), in0=over_fine(coarse_hd), in1=over_coarse(fine_tl), op=ALU.mult
+        nc.gpsimd.tensor_tensor(out=fine_all[:], in0=fine_hd[:], in1=fine_tl[:], op=ALU.add)
+        nc.gpsimd.tensor_tensor(
+            out=as_grid(cross2), in0=over_fine(coarse_tl, 0, FAST_COARSE),
+            in1=over_coarse(fine_all, FAST_COARSE), op=ALU.mult,
         )
         nc.vector.tensor_tensor(
-            out=as_grid(cross2), in0=over_fine(coarse_tl), in1=over_coarse(fine_all), op=ALU.mult
+            out=as_grid(cross), in0=over_fine(coarse_hd, 0, FAST_COARSE),
+            in1=over_coarse(fine_tl, FAST_COARSE), op=ALU.mult,
         )
-        nc.vector.tensor_tensor(out=cross[:], in0=cross[:], in1=cross2[:], op=ALU.add)
         nc.vector.tensor_tensor(out=product[:], in0=product[:], in1=f_head[:], op=ALU.subtract)
-        nc.vector.tensor_tensor(out=f_tail[:], in0=product[:], in1=cross[:], op=ALU.add)
+        nc.vector.tensor_tensor(out=cross[:], in0=product[:], in1=cross[:], op=ALU.add)
+        nc.vector.tensor_tensor(out=f_tail[:], in0=cross[:], in1=cross2[:], op=ALU.add)
 
-        cols = keep.tile([P, 3 * CHUNKS], F32)
-        nc.vector.tensor_copy(
-            out=cols[:].rearrange("p (v c) -> p v c", v=3), in_=vectors[:, :, 0:CHUNKS]
-        )
         b_wide = keep.tile([P, CHUNKS, P], F32)
-        nc.vector.tensor_copy(
-            out=b_wide[:], in_=cols[:, 0:CHUNKS].unsqueeze(2).to_broadcast([P, CHUNKS, P])
+        nc.gpsimd.tensor_scalar(
+            out=b_wide[:], in0=vectors[:, 0, 0:CHUNKS].unsqueeze(2).to_broadcast([P, CHUNKS, P]),
+            scalar1=1.0, scalar2=0.0, op0=ALU.mult, op1=ALU.add,
+        )
+        nc.gpsimd.tensor_tensor(out=coarse_all[:], in0=coarse_hd[:], in1=coarse_tl[:], op=ALU.add)
+        nc.gpsimd.tensor_tensor(
+            out=as_grid(f_slow), in0=over_fine(coarse_all, SLOW_FROM, COARSE),
+            in1=over_coarse(fine_all, COARSE - SLOW_FROM), op=ALU.mult,
+        )
+        angle = keep.tile([P, N_POS], F32)
+        nc.gpsimd.tensor_scalar(
+            out=angle[:], in0=pos[:], scalar1=2.0 * math.pi, scalar2=0.0, op0=ALU.mult, op1=ALU.add
+        )
+        minus_angle = keep.tile([P, N_POS], F32)
+        nc.gpsimd.tensor_scalar(
+            out=minus_angle[:], in0=pos[:], scalar1=-2.0 * math.pi, scalar2=0.0, op0=ALU.mult, op1=ALU.add
         )
 
         w_emb = keep.tile([P, D], BF16)
-        nc.scalar.copy(
-            out=w_emb[:].rearrange("f (g t p) -> f g t p", g=PASSES, t=PACK),
-            in_=w_emb_raw[:].rearrange("f (g p t) -> f g t p", g=PASSES, t=PACK),
-        )
+        for g in range(PASSES):
+            span = slice(g * K_PASS, (g + 1) * K_PASS)
+            nc.scalar.copy(
+                out=w_emb[:, span].rearrange("f (t p) -> f t p", t=PACK),
+                in_=w_emb_raw[:, span].rearrange("f (p t) -> f t p", t=PACK),
+            )
 
         w_codes = keep.tile([P, PASSES, N_ALL], U32, align_bytes=64)
         w_scales = keep.tile([P, PASSES, N_ALL], U8, align_bytes=64)
 
         def regroup_weight(w):
             w_grouped = work.tile([P, PASSES, N_OUT, PACK], BF16, bufs=2, align_bytes=64)
-            nc.scalar.copy(out=w_grouped[:], in_=w_raw[w][:].rearrange("p g t n -> p g n t"))
+            src = w_raw[w][:].rearrange("p g t n -> p g n t")
+            nc.gpsimd.tensor_scalar(
+                out=w_grouped[:], in0=src, scalar1=1.0, scalar2=0.0, op0=ALU.mult, op1=ALU.add
+            )
             return w_grouped
 
         def quantise_weight(w, w_grouped):
@@ -186,34 +220,51 @@ def tile_ffnn_encoder_pa_t_kernel(
                     in_=w_grouped[:, g].rearrange("p n t -> p (n t)"),
                 )
 
-        timing = keep.tile([P, N_POS, D], F32)
+        timing = keep.tile([P, N_POS, 2, PACK, P], F32)
 
-        def make_timing(a):
+        def make_turns(a):
+            fast = fast_quads(a)
             here = pos[:, a : a + 1]
-            turns = work.tile([P, N_FREQ], F32, bufs=2)
+            shape = [P, PACK, fast]
+            turns = work.tile(shape, F32, bufs=2)
             nc.vector.tensor_scalar(
-                out=turns[:], in0=f_head[:], scalar1=here, scalar2=-0.125, op0=ALU.mult, op1=ALU.add
+                out=turns[:], in0=f_head[:, :, 0:fast], scalar1=here, scalar2=-0.125,
+                op0=ALU.mult, op1=ALU.add,
             )
-            whole = work.tile([P, N_FREQ], F32, bufs=2)
+            whole = work.tile(shape, F32, bufs=2)
             nc.vector.tensor_scalar(
                 out=whole[:], in0=turns[:], scalar1=ROUND_TO_INT, scalar2=ROUND_TO_INT,
                 op0=ALU.add, op1=ALU.subtract,
             )
             nc.vector.tensor_tensor(out=whole[:], in0=turns[:], in1=whole[:], op=ALU.subtract)
-            frac = work.tile([P, N_FREQ], F32, bufs=2)
+            frac = work.tile(shape, F32, bufs=2)
             nc.vector.scalar_tensor_tensor(
-                out=frac[:], in0=f_tail[:], scalar=here, in1=whole[:], op0=ALU.mult, op1=ALU.add
+                out=frac[:], in0=f_tail[:, :, 0:fast], scalar=here, in1=whole[:],
+                op0=ALU.mult, op1=ALU.add,
             )
-            distance = work.tile([P, D], F32, bufs=2)
+            return frac
+
+        def fast_signal(a, frac):
+            fast = fast_quads(a)
+            distance = work.tile([P, 2, PACK, fast], F32, bufs=2)
+            for half, shift in enumerate((minus_eighth, plus_eighth)):
+                nc.scalar.activation(
+                    out=distance[:, half], in_=frac[:], func=FUNC.Abs, bias=shift[:], scale=1.0
+                )
             nc.scalar.activation(
-                out=distance[:, 0:N_FREQ], in_=frac[:], func=FUNC.Abs, bias=minus_eighth[:], scale=1.0
-            )
-            nc.scalar.activation(
-                out=distance[:, N_FREQ:D], in_=frac[:], func=FUNC.Abs, bias=plus_eighth[:], scale=1.0
-            )
-            nc.scalar.activation(
-                out=timing[:, a, :], in_=distance[:], func=FUNC.Sin,
+                out=timing[:, a, :, :, 0:fast], in_=distance[:], func=FUNC.Sin,
                 bias=quarter_turn[:], scale=-2.0 * math.pi,
+            )
+
+        def slow_signal(a):
+            fast = fast_quads(a)
+            f_here = f_slow[:, :, fast - SLOW_FROM * QUADS :]
+            nc.scalar.activation(
+                out=timing[:, a, 0, :, fast:P], in_=f_here, func=FUNC.Sin, scale=angle[:, a : a + 1]
+            )
+            nc.scalar.activation(
+                out=timing[:, a, 1, :, fast:P], in_=f_here, func=FUNC.Sin,
+                bias=quarter_turn[:], scale=minus_angle[:, a : a + 1],
             )
 
         def transpose_x(a):
@@ -226,7 +277,7 @@ def tile_ffnn_encoder_pa_t_kernel(
             nc.scalar.copy(out=x_t[:], in_=x_t_ps[:])
             return x_t
 
-        def embed_bank(a, b, half, x_t, e, sum_e):
+        def embed_bank(b, half, x_t):
             z = psum_z.tile([P, BANK], F32)
             for j in range(BANK // P):
                 nc.tensor.matmul(
@@ -244,11 +295,14 @@ def tile_ffnn_encoder_pa_t_kernel(
                 start=False,
                 stop=True,
             )
+            return z
+
+        def add_timing(a, b, half, z, e, sum_e):
             nc.vector.scalar_tensor_tensor(
                 out=e[:, half * BANK : (half + 1) * BANK],
                 in0=z[:],
                 scalar=0.0,
-                in1=timing[:, a, half * BANK : (half + 1) * BANK],
+                in1=timing[:, a, half].rearrange("p t q -> p (t q)"),
                 op0=ALU.max,
                 op1=ALU.add,
                 accum_out=sum_e[:, b, half : half + 1],
@@ -260,7 +314,7 @@ def tile_ffnn_encoder_pa_t_kernel(
                 out=squares[:], in_=e[:], func=FUNC.Square, accum_out=sum_sq[:, b : b + 1]
             )
 
-        def normalise(e_tiles, sum_e, sum_sq):
+        def statistics(sum_e, sum_sq):
             total = work.tile([P, BATCH], F32, bufs=2)
             nc.gpsimd.tensor_tensor(out=total[:], in0=sum_e[:, :, 0], in1=sum_e[:, :, 1], op=ALU.add)
             minus_mean = work.tile([P, BATCH], F32, bufs=2)
@@ -278,15 +332,15 @@ def tile_ffnn_encoder_pa_t_kernel(
             nc.gpsimd.tensor_tensor(out=rstd[:], in0=var_eps[:], in1=minus_half[:], op=ALU.pow)
             shift = work.tile([P, BATCH], F32, bufs=2)
             nc.gpsimd.tensor_tensor(out=shift[:], in0=minus_mean[:], in1=rstd[:], op=ALU.mult)
-            normed_tiles = []
-            for b in range(BATCH):
-                normed = work.tile([P, D], F32, name="normed%d" % b, tag="normed", bufs=8)
-                nc.gpsimd.tensor_scalar(
-                    out=normed[:], in0=e_tiles[b][:], scalar1=rstd[:, b : b + 1],
-                    scalar2=shift[:, b : b + 1], op0=ALU.mult, op1=ALU.add,
-                )
-                normed_tiles.append(normed)
-            return normed_tiles
+            return rstd, shift
+
+        def normalise(b, e, rstd, shift):
+            normed = work.tile([P, D], F32, bufs=8)
+            nc.gpsimd.tensor_scalar(
+                out=normed[:], in0=e[:], scalar1=rstd[:, b : b + 1],
+                scalar2=shift[:, b : b + 1], op0=ALU.mult, op1=ALU.add,
+            )
+            return normed
 
         def scale_and_shift(normed_tiles, c, planes):
             normed_t = psum_t.tile([P, GROUP], F32, tag="tp")
@@ -317,14 +371,15 @@ def tile_ffnn_encoder_pa_t_kernel(
             )
             return codes, scales
 
-        def project(b, h_mx, result):
+        def project(b, h_mx, acc_v):
             tokens = slice(b * P, (b + 1) * P)
-            for name, first, width in (("acc_qk", 0, BANK), ("acc_v", BANK, N_ALL - BANK)):
-                acc = psum_o.tile([P, width], F32, name=name, tag=name)
+            acc_qk = psum_o.tile([P, BANK], F32)
+            half_v = acc_v[:, b % 2, :]
+            for acc, first, width in ((acc_qk[:], 0, BANK), (half_v, BANK, N_OUT)):
                 for g in range(PASSES):
                     codes, scales = h_mx[g]
                     nc.tensor.matmul_mx(
-                        out=acc[:],
+                        out=acc,
                         lhsT=codes[:, tokens].bitcast(FP8X4),
                         lhsT_scale=scales[:, tokens],
                         rhs=w_codes[:, g, first : first + width].bitcast(FP8X4),
@@ -332,29 +387,46 @@ def tile_ffnn_encoder_pa_t_kernel(
                         start=(g == 0),
                         stop=(g == PASSES - 1),
                     )
+            return acc_qk
+
+        def add_bias(b, acc_qk, acc_v, result):
+            nc.vector.tensor_tensor(
+                out=result[:, b, 0:BANK], in0=acc_qk[:], in1=bias_qkv[:, 0:BANK], op=ALU.add
+            )
+            if b % 2 == 1:
                 nc.vector.tensor_tensor(
-                    out=result[:, b, first : first + width], in0=acc[:],
-                    in1=bias_qkv[:, first : first + width], op=ALU.add,
+                    out=result[:, b - 1 : b + 1, BANK:N_ALL],
+                    in0=acc_v[:],
+                    in1=bias_qkv[:, BANK:N_ALL].unsqueeze(1).to_broadcast([P, 2, N_OUT]),
+                    op=ALU.add,
                 )
 
-        NORM_AT = BATCH
-        CHUNKS_AT = 2 * BATCH
-        PROJECT_AT = 3 * BATCH + 1
-        CHUNKS_A_STEP = CHUNKS // BATCH
+        NORM_AT = 4
+        TURN_AT = 7
+        QUANT_AT = 11
+        PROJECT_AT = 12
 
         def group_at(step, lag):
             group, place = divmod(step - lag, BATCH)
             return (group if 0 <= group < N_POS else None), place
 
+        cols = keep.tile([P, 3 * CHUNKS], F32)
         x_t_of = {0: transpose_x(0)}
-        make_timing(0)
+        z_of_tile = [embed_bank(0, half, x_t_of[0]) for half in range(HALVES)]
+        slow_signal(0)
+        fast_signal(0, make_turns(0))
+        x_t_of[1] = transpose_x(1)
+        nc.gpsimd.tensor_copy(
+            out=cols[:].rearrange("p (v c) -> p v c", v=3), in_=vectors[:, :, 0:CHUNKS]
+        )
         sums_of = {}
         e_of = {}
         normed_of = {}
+        stats_of = {}
+        planes_of = {}
         h_mx_of = {}
-        w_grouped_of = {}
-        waiting = None
-        for step in range(BATCH * N_POS + PROJECT_AT):
+        projected = None
+        for step in range(BATCH * N_POS + PROJECT_AT + 1):
             group, b = group_at(step, 0)
             if group is not None:
                 if b == 0:
@@ -365,48 +437,76 @@ def tile_ffnn_encoder_pa_t_kernel(
                 e = work.tile([P, D], F32, bufs=8)
                 e_of[group].append(e)
                 for half in range(HALVES):
-                    embed_bank(group, b, half, x_t_of[group], e, sums_of[group][0])
-            if step + 1 < N_POS:
-                make_timing(step + 1)
-
+                    add_timing(group, b, half, z_of_tile[half], e, sums_of[group][0])
+            t_a = step + 1 if step + 1 < N_POS else None
+            if t_a is not None:
+                slow_signal(t_a)
+                frac_now = make_turns(t_a)
+            w, at = divmod(step - 4, 2)
+            if 0 <= w < 3 and at == 0:
+                w_grouped = regroup_weight(w)
             done, place = group_at(step, NORM_AT)
             if done is not None and place == 0:
-                normed_of[done] = normalise(e_of[done], sums_of[done][0], sums_of[done][1])
-            if group is not None and b == 1 and 1 <= group <= 3:
-                quantise_weight(group - 1, w_grouped_of[group - 1])
+                stats_of[done] = statistics(sums_of[done][0], sums_of[done][1])
+                normed_of[done] = []
+                for bb in range(BATCH):
+                    normed_of[done].append(normalise(bb, e_of[done][bb], stats_of[done][0], stats_of[done][1]))
+            if 0 <= w < 3 and at == 1:
+                quantise_weight(w, w_grouped)
 
-            grouped = None
-            if waiting is not None:
-                grouped = regroup(waiting[1])
-            turned, j = group_at(step, CHUNKS_AT)
-            if turned is not None:
-                for c in range(j * CHUNKS_A_STEP, (j + 1) * CHUNKS_A_STEP):
-                    if c == 0:
-                        h_mx_of[turned] = []
-                    if c % PACK == 0:
-                        planes = work.tile([P, PACK, GROUP], BF16, bufs=2)
-                    scale_and_shift(normed_of[turned], c, planes)
+            def drain():
+                if projected is not None:
+                    of_group, of_b, acc_qk, acc_v_of = projected
+                    add_bias(of_b, acc_qk, acc_v_of, results[of_group])
+                    if of_b == BATCH - 1:
+                        for w, out in enumerate((out_0, out_1, out_2)):
+                            nc.sync.dma_start(
+                                out=out.rearrange("b (a p) n -> a p b n", p=P)[of_group],
+                                in_=results[of_group][:, :, w * N_OUT : (w + 1) * N_OUT],
+                            )
 
-            if group is not None:
-                sum_of_squares(e, b, sums_of[group][1])
-                if b == 2 and group + 1 < N_POS:
-                    x_t_of[group + 1] = transpose_x(group + 1)
-                if b == 3 and group < 3:
-                    w_grouped_of[group] = regroup_weight(group)
+            if projected is not None and projected[1] == 0:
+                result = work.tile([P, BATCH, N_ALL], F32, bufs=2)
+                if projected[0] == 0:
+                    results = {}
+                results[projected[0]] = result
+            quantised, place = group_at(step, QUANT_AT)
+            if quantised is not None and place == 0:
+                grouped = [regroup(p) for p in planes_of[quantised]]
+                drain()
+                h_mx_of[quantised] = [quantise(g) for g in grouped]
+            else:
+                drain()
+            projected = None
 
+            following, next_b = group_at(step + 1, 0)
             ready, tile_b = group_at(step, PROJECT_AT)
-            if ready is not None:
-                if tile_b == 0:
-                    result = work.tile([P, BATCH, N_ALL], F32, bufs=2)
-                project(tile_b, h_mx_of[ready], result)
-                if tile_b == BATCH - 1:
-                    for w, out in enumerate((out_0, out_1, out_2)):
-                        nc.sync.dma_start(
-                            out=out.rearrange("b (a p) n -> a p b n", p=P)[ready],
-                            in_=result[:, :, w * N_OUT : (w + 1) * N_OUT],
-                        )
-            if grouped is not None:
-                h_mx_of[waiting[0]].append(quantise(grouped))
-                waiting = None
-            if turned is not None and (j + 1) * CHUNKS_A_STEP % PACK == 0:
-                waiting = (turned, planes)
+            turned, place = group_at(step, TURN_AT)
+            if turned is not None and place == 0:
+                planes_of[turned] = []
+                for c in range(CHUNKS):
+                    if c % PACK == 0:
+                        planes = work.tile([P, PACK, GROUP], BF16, bufs=4)
+                        planes_of[turned].append(planes)
+                    scale_and_shift(normed_of[turned], c, planes)
+                    if c == 2 and following is not None:
+                        z_of_tile = [embed_bank(next_b, half, x_t_of[following]) for half in range(HALVES)]
+                    if c == 3 and group is not None:
+                        sum_of_squares(e, b, sums_of[group][1])
+                    if c == 3 and ready is not None:
+                        if tile_b % 2 == 0:
+                            acc_v = psum_o.tile([P, 2, N_OUT], F32, bufs=1)
+                        projected = (ready, tile_b, project(tile_b, h_mx_of[ready], acc_v), acc_v)
+            else:
+                if following is not None:
+                    z_of_tile = [embed_bank(next_b, half, x_t_of[following]) for half in range(HALVES)]
+                if group is not None:
+                    sum_of_squares(e, b, sums_of[group][1])
+                if ready is not None:
+                    if tile_b % 2 == 0:
+                        acc_v = psum_o.tile([P, 2, N_OUT], F32, bufs=1)
+                    projected = (ready, tile_b, project(tile_b, h_mx_of[ready], acc_v), acc_v)
+            if t_a is not None:
+                fast_signal(t_a, frac_now)
+            if group is not None and b == 0 and group + 2 < N_POS:
+                x_t_of[group + 2] = transpose_x(group + 2)

@@ -237,7 +237,7 @@ def tile_ffnn_encoder_pa_t_kernel(
                 op0=ALU.add, op1=ALU.subtract,
             )
             nc.vector.tensor_tensor(out=whole[:], in0=turns[:], in1=whole[:], op=ALU.subtract)
-            frac = work.tile(shape, F32, bufs=2)
+            frac = work.tile(shape, F32, bufs=4)
             nc.vector.scalar_tensor_tensor(
                 out=frac[:], in0=f_tail[:, :, 0:fast], scalar=here, in1=whole[:],
                 op0=ALU.mult, op1=ALU.add,
@@ -334,13 +334,11 @@ def tile_ffnn_encoder_pa_t_kernel(
             nc.gpsimd.tensor_tensor(out=shift[:], in0=minus_mean[:], in1=rstd[:], op=ALU.mult)
             return rstd, shift
 
-        def normalise(b, e, rstd, shift):
-            normed = work.tile([P, D], F32, bufs=8)
-            nc.gpsimd.tensor_scalar(
-                out=normed[:], in0=e[:], scalar1=rstd[:, b : b + 1],
+        def normalise(engine, b, e, rstd, shift):
+            engine.tensor_scalar(
+                out=e[:], in0=e[:], scalar1=rstd[:, b : b + 1],
                 scalar2=shift[:, b : b + 1], op0=ALU.mult, op1=ALU.add,
             )
-            return normed
 
         def scale_and_shift(normed_tiles, c, planes):
             normed_t = psum_t.tile([P, GROUP], F32, tag="tp")
@@ -351,14 +349,19 @@ def tile_ffnn_encoder_pa_t_kernel(
                     identity=ident_f[:],
                 )
             nc.scalar.activation(
-                out=planes[:, c % PACK, :], in_=normed_t[:], func=FUNC.Identity,
+                out=planes[:, c % PACK // 2, :, c % 2], in_=normed_t[:], func=FUNC.Identity,
                 scale=cols[:, CHUNKS + c : CHUNKS + c + 1],
                 bias=cols[:, 2 * CHUNKS + c : 2 * CHUNKS + c + 1],
             )
 
         def regroup(planes):
             grouped = work.tile([P, GROUP, PACK], BF16, bufs=2, align_bytes=64)
-            nc.vector.tensor_copy(out=grouped[:], in_=planes[:].rearrange("p t r -> p r t"))
+            nc.vector.tensor_copy(
+                out=grouped[:].rearrange("p r t -> p (r t)").bitcast(F32)
+                .rearrange("p (r u) -> p r u", u=PACK // 2),
+                in_=planes[:].rearrange("p u r e -> p (u r e)").bitcast(F32)
+                .rearrange("p (u r) -> p r u", u=PACK // 2),
+            )
             return grouped
 
         def quantise(grouped):
@@ -401,10 +404,14 @@ def tile_ffnn_encoder_pa_t_kernel(
                     op=ALU.add,
                 )
 
-        NORM_AT = 4
-        TURN_AT = 7
-        QUANT_AT = 11
-        PROJECT_AT = 12
+        STATS_AT = 5
+        NORM_AT = 6
+        TURN_AT = 8
+        QUANT_AT = 12
+        PROJECT_AT = 16
+        CHUNKS_A_STEP = CHUNKS // BATCH
+        WEIGHTS_AT = 6
+        WEIGHT_LAG = 2
 
         def group_at(step, lag):
             group, place = divmod(step - lag, BATCH)
@@ -416,15 +423,16 @@ def tile_ffnn_encoder_pa_t_kernel(
         slow_signal(0)
         fast_signal(0, make_turns(0))
         x_t_of[1] = transpose_x(1)
+        frac_of = {1: make_turns(1), 2: make_turns(2)}
         nc.gpsimd.tensor_copy(
             out=cols[:].rearrange("p (v c) -> p v c", v=3), in_=vectors[:, :, 0:CHUNKS]
         )
         sums_of = {}
         e_of = {}
-        normed_of = {}
         stats_of = {}
         planes_of = {}
         h_mx_of = {}
+        w_grouped_of = {}
         projected = None
         for step in range(BATCH * N_POS + PROJECT_AT + 1):
             group, b = group_at(step, 0)
@@ -434,79 +442,80 @@ def tile_ffnn_encoder_pa_t_kernel(
                     sum_sq = work.tile([P, BATCH], F32, bufs=3)
                     sums_of[group] = (sum_e, sum_sq)
                     e_of[group] = []
-                e = work.tile([P, D], F32, bufs=8)
+                e = work.tile([P, D], F32, bufs=16)
                 e_of[group].append(e)
                 for half in range(HALVES):
                     add_timing(group, b, half, z_of_tile[half], e, sums_of[group][0])
-            t_a = step + 1 if step + 1 < N_POS else None
-            if t_a is not None:
-                slow_signal(t_a)
-                frac_now = make_turns(t_a)
-            w, at = divmod(step - 4, 2)
-            if 0 <= w < 3 and at == 0:
-                w_grouped = regroup_weight(w)
-            done, place = group_at(step, NORM_AT)
+
+            done, place = group_at(step, STATS_AT)
             if done is not None and place == 0:
                 stats_of[done] = statistics(sums_of[done][0], sums_of[done][1])
-                normed_of[done] = []
-                for bb in range(BATCH):
-                    normed_of[done].append(normalise(bb, e_of[done][bb], stats_of[done][0], stats_of[done][1]))
-            if 0 <= w < 3 and at == 1:
-                quantise_weight(w, w_grouped)
+                for tile_b in (2, 3):
+                    normalise(nc.gpsimd, tile_b, e_of[done][tile_b], *stats_of[done])
 
-            def drain():
-                if projected is not None:
-                    of_group, of_b, acc_qk, acc_v_of = projected
-                    add_bias(of_b, acc_qk, acc_v_of, results[of_group])
-                    if of_b == BATCH - 1:
-                        for w, out in enumerate((out_0, out_1, out_2)):
-                            nc.sync.dma_start(
-                                out=out.rearrange("b (a p) n -> a p b n", p=P)[of_group],
-                                in_=results[of_group][:, :, w * N_OUT : (w + 1) * N_OUT],
-                            )
-
-            if projected is not None and projected[1] == 0:
-                result = work.tile([P, BATCH, N_ALL], F32, bufs=2)
-                if projected[0] == 0:
-                    results = {}
-                results[projected[0]] = result
+            grouped = None
             quantised, place = group_at(step, QUANT_AT)
-            if quantised is not None and place == 0:
-                grouped = [regroup(p) for p in planes_of[quantised]]
-                drain()
-                h_mx_of[quantised] = [quantise(g) for g in grouped]
-            else:
-                drain()
-            projected = None
+            g, odd = divmod(place, 2)
+            if quantised is not None and odd == 0:
+                grouped = regroup(planes_of[quantised][g])
+            done, place = group_at(step, NORM_AT)
+            if done is not None and place == 0:
+                for tile_b in (0, 1):
+                    normalise(nc.vector, tile_b, e_of[done][tile_b], *stats_of[done])
+
+            turned, j = group_at(step, TURN_AT)
+            if turned is not None:
+                c = j * CHUNKS_A_STEP
+                if c == 0:
+                    planes_of[turned] = []
+                if c % PACK == 0:
+                    planes = work.tile([P, PACK // 2, GROUP, 2], BF16, bufs=4)
+                    planes_of[turned].append(planes)
+                scale_and_shift(e_of[turned], c, planes)
+
+            if projected is not None:
+                of_group, of_b, acc_qk, acc_v_of = projected
+                if of_b == 0:
+                    result = work.tile([P, BATCH, N_ALL], F32, bufs=2)
+                add_bias(of_b, acc_qk, acc_v_of, result)
+                if of_b == BATCH - 1:
+                    for w, out in enumerate((out_0, out_1, out_2)):
+                        nc.sync.dma_start(
+                            out=out.rearrange("b (a p) n -> a p b n", p=P)[of_group],
+                            in_=result[:, :, w * N_OUT : (w + 1) * N_OUT],
+                        )
+                projected = None
+
+            signalled = step + 1
+            if signalled < N_POS:
+                fast_signal(signalled, frac_of[signalled])
+            if grouped is not None:
+                if g == 0:
+                    h_mx_of[quantised] = []
+                h_mx_of[quantised].append(quantise(grouped))
+            if group is not None:
+                sum_of_squares(e, b, sums_of[group][1])
+
+            w = step - WEIGHTS_AT
+            if 0 <= w < 3:
+                w_grouped_of[w] = regroup_weight(w)
+            w = step - WEIGHTS_AT - WEIGHT_LAG
+            if 0 <= w < 3:
+                quantise_weight(w, w_grouped_of[w])
 
             following, next_b = group_at(step + 1, 0)
+            if following is not None:
+                z_of_tile = [embed_bank(next_b, half, x_t_of[following]) for half in range(HALVES)]
+            if turned is not None:
+                scale_and_shift(e_of[turned], c + 1, planes)
+            if signalled < N_POS:
+                slow_signal(signalled)
+            if signalled + 2 < N_POS:
+                frac_of[signalled + 2] = make_turns(signalled + 2)
             ready, tile_b = group_at(step, PROJECT_AT)
-            turned, place = group_at(step, TURN_AT)
-            if turned is not None and place == 0:
-                planes_of[turned] = []
-                for c in range(CHUNKS):
-                    if c % PACK == 0:
-                        planes = work.tile([P, PACK, GROUP], BF16, bufs=4)
-                        planes_of[turned].append(planes)
-                    scale_and_shift(normed_of[turned], c, planes)
-                    if c == 2 and following is not None:
-                        z_of_tile = [embed_bank(next_b, half, x_t_of[following]) for half in range(HALVES)]
-                    if c == 3 and group is not None:
-                        sum_of_squares(e, b, sums_of[group][1])
-                    if c == 3 and ready is not None:
-                        if tile_b % 2 == 0:
-                            acc_v = psum_o.tile([P, 2, N_OUT], F32, bufs=1)
-                        projected = (ready, tile_b, project(tile_b, h_mx_of[ready], acc_v), acc_v)
-            else:
-                if following is not None:
-                    z_of_tile = [embed_bank(next_b, half, x_t_of[following]) for half in range(HALVES)]
-                if group is not None:
-                    sum_of_squares(e, b, sums_of[group][1])
-                if ready is not None:
-                    if tile_b % 2 == 0:
-                        acc_v = psum_o.tile([P, 2, N_OUT], F32, bufs=1)
-                    projected = (ready, tile_b, project(tile_b, h_mx_of[ready], acc_v), acc_v)
-            if t_a is not None:
-                fast_signal(t_a, frac_now)
-            if group is not None and b == 0 and group + 2 < N_POS:
+            if ready is not None:
+                if tile_b % 2 == 0:
+                    acc_v = psum_o.tile([P, 2, N_OUT], F32, bufs=1)
+                projected = (ready, tile_b, project(tile_b, h_mx_of[ready], acc_v), acc_v)
+            if group is not None and b == 2 and group + 2 < N_POS:
                 x_t_of[group + 2] = transpose_x(group + 2)

@@ -18,6 +18,7 @@ BATCH = 4
 SEQ = 1024
 FIN = 128
 D = 1024
+ROOT_D = 32
 N_OUT = 256
 N_ALL = 3 * N_OUT
 EPS = 1e-3
@@ -103,6 +104,8 @@ def tile_ffnn_encoder_pa_t_kernel(
         nc.vector.memset(one[:], 1.0)
         warm = keep.tile([P, 1], F32)
         nc.scalar.activation(out=warm[:], in_=one[:], func=FUNC.Sin)
+        quarter_turn = keep.tile([P, 1], F32)
+        nc.scalar.mul(out=quarter_turn[:], in_=one[:], mul=0.5 * math.pi)
         ident_b = keep.tile([P, P], BF16)
         make_identity(nc, ident_b[:])
         coarse_hd = keep.tile([P, COARSE], F32)
@@ -115,23 +118,40 @@ def tile_ffnn_encoder_pa_t_kernel(
             nc.vector.memset(coarse_hd[:, i : i + 1], head_of(value))
             nc.scalar.mul(out=coarse_tl[:, i : i + 1], in_=one[:], mul=value - head_of(value))
         for i, value in enumerate(fine_values):
-            nc.gpsimd.memset(fine_hd[:, i : i + 1], head_of(value))
-            nc.vector.tensor_scalar_mul(fine_tl[:, i : i + 1], one[:], value - head_of(value))
-        ident_f = keep.tile([P, P], F32)
-        make_identity(nc, ident_f[:])
-        minus_eighth = keep.tile([P, 1], F32)
-        nc.gpsimd.memset(minus_eighth[:], -0.125)
-        plus_eighth = keep.tile([P, 1], F32)
-        nc.gpsimd.memset(plus_eighth[:], 0.125)
-        minus_half = keep.tile([P, BATCH], F32)
-        nc.gpsimd.memset(minus_half[:], -0.5)
+            head = fine_hd[:, i : i + 1]
+            tail = fine_tl[:, i : i + 1]
+            if i < FINE // 2:
+                nc.vector.memset(head, head_of(value))
+                nc.vector.tensor_scalar_mul(tail, one[:], value - head_of(value))
+            else:
+                nc.gpsimd.memset(head, head_of(value))
+                nc.scalar.mul(out=tail, in_=one[:], mul=value - head_of(value))
         pos = keep.tile([P, N_POS], F32)
         nc.gpsimd.iota(
             out=pos[:], pattern=[[P, N_POS]], base=0, channel_multiplier=1,
             allow_small_or_imprecise_dtypes=True,
         )
-        quarter_turn = keep.tile([P, 1], F32)
-        nc.scalar.mul(out=quarter_turn[:], in_=one[:], mul=0.5 * math.pi)
+        angle = keep.tile([P, N_POS], F32)
+        nc.gpsimd.tensor_scalar(
+            out=angle[:], in0=pos[:], scalar1=2.0 * math.pi, scalar2=0.0, op0=ALU.mult, op1=ALU.add
+        )
+        minus_angle = keep.tile([P, N_POS], F32)
+        nc.gpsimd.tensor_scalar(
+            out=minus_angle[:], in0=pos[:], scalar1=-2.0 * math.pi, scalar2=0.0, op0=ALU.mult, op1=ALU.add
+        )
+        minus_eighth = keep.tile([P, 1], F32)
+        nc.gpsimd.memset(minus_eighth[:], -0.125)
+        plus_eighth = keep.tile([P, 1], F32)
+        nc.gpsimd.memset(plus_eighth[:], 0.125)
+        ident_f = keep.tile([P, P], F32)
+        make_identity(nc, ident_f[:])
+        b_wide = keep.tile([P, CHUNKS, P], F32)
+        nc.gpsimd.tensor_scalar(
+            out=b_wide[:], in0=vectors[:, 0, 0:CHUNKS].unsqueeze(2).to_broadcast([P, CHUNKS, P]),
+            scalar1=1.0, scalar2=0.0, op0=ALU.mult, op1=ALU.add,
+        )
+        minus_half = keep.tile([P, BATCH], F32)
+        nc.gpsimd.memset(minus_half[:], -0.5)
 
         def over_fine(table, first, last):
             cells = table[:, first:last].unsqueeze(2).unsqueeze(3)
@@ -160,37 +180,52 @@ def tile_ffnn_encoder_pa_t_kernel(
         nc.vector.tensor_single_scalar(
             out=f_head[:].bitcast(I32), in_=product[:].bitcast(I32), scalar=-2048, op=ALU.bitwise_and
         )
-        nc.gpsimd.tensor_tensor(out=fine_all[:], in0=fine_hd[:], in1=fine_tl[:], op=ALU.add)
-        nc.gpsimd.tensor_tensor(
-            out=as_grid(cross2), in0=over_fine(coarse_tl, 0, FAST_COARSE),
-            in1=over_coarse(fine_all, FAST_COARSE), op=ALU.mult,
+        def make_turns(a):
+            fast = fast_quads(a)
+            here = pos[:, a : a + 1]
+            shape = [P, PACK, fast]
+            turns = work.tile(shape, F32, bufs=2)
+            nc.vector.tensor_scalar(
+                out=turns[:], in0=f_head[:, :, 0:fast], scalar1=here, scalar2=-0.125,
+                op0=ALU.mult, op1=ALU.add,
+            )
+            whole = work.tile(shape, F32, bufs=2)
+            nc.vector.tensor_scalar(
+                out=whole[:], in0=turns[:], scalar1=ROUND_TO_INT, scalar2=ROUND_TO_INT,
+                op0=ALU.add, op1=ALU.subtract,
+            )
+            nc.vector.tensor_tensor(out=whole[:], in0=turns[:], in1=whole[:], op=ALU.subtract)
+            return whole
+
+        def add_tail(a, whole):
+            fast = fast_quads(a)
+            frac = work.tile([P, PACK, fast], F32, bufs=4)
+            nc.vector.scalar_tensor_tensor(
+                out=frac[:], in0=f_tail[:, :, 0:fast], scalar=pos[:, a : a + 1], in1=whole[:],
+                op0=ALU.mult, op1=ALU.add,
+            )
+            return frac
+
+        frac_of = {}
+        turns_of = {0: make_turns(0)}
+        nc.vector.tensor_tensor(out=coarse_all[:], in0=coarse_hd[:], in1=coarse_tl[:], op=ALU.add)
+        nc.vector.tensor_tensor(out=fine_all[:], in0=fine_hd[:], in1=fine_tl[:], op=ALU.add)
+        nc.vector.tensor_tensor(
+            out=as_grid(f_slow), in0=over_fine(coarse_all, SLOW_FROM, COARSE),
+            in1=over_coarse(fine_all, COARSE - SLOW_FROM), op=ALU.mult,
         )
         nc.vector.tensor_tensor(
             out=as_grid(cross), in0=over_fine(coarse_hd, 0, FAST_COARSE),
             in1=over_coarse(fine_tl, FAST_COARSE), op=ALU.mult,
         )
         nc.vector.tensor_tensor(out=product[:], in0=product[:], in1=f_head[:], op=ALU.subtract)
+        nc.vector.tensor_tensor(
+            out=as_grid(cross2), in0=over_fine(coarse_tl, 0, FAST_COARSE),
+            in1=over_coarse(fine_all, FAST_COARSE), op=ALU.mult,
+        )
         nc.vector.tensor_tensor(out=cross[:], in0=product[:], in1=cross[:], op=ALU.add)
         nc.vector.tensor_tensor(out=f_tail[:], in0=cross[:], in1=cross2[:], op=ALU.add)
-
-        b_wide = keep.tile([P, CHUNKS, P], F32)
-        nc.gpsimd.tensor_scalar(
-            out=b_wide[:], in0=vectors[:, 0, 0:CHUNKS].unsqueeze(2).to_broadcast([P, CHUNKS, P]),
-            scalar1=1.0, scalar2=0.0, op0=ALU.mult, op1=ALU.add,
-        )
-        nc.gpsimd.tensor_tensor(out=coarse_all[:], in0=coarse_hd[:], in1=coarse_tl[:], op=ALU.add)
-        nc.gpsimd.tensor_tensor(
-            out=as_grid(f_slow), in0=over_fine(coarse_all, SLOW_FROM, COARSE),
-            in1=over_coarse(fine_all, COARSE - SLOW_FROM), op=ALU.mult,
-        )
-        angle = keep.tile([P, N_POS], F32)
-        nc.gpsimd.tensor_scalar(
-            out=angle[:], in0=pos[:], scalar1=2.0 * math.pi, scalar2=0.0, op0=ALU.mult, op1=ALU.add
-        )
-        minus_angle = keep.tile([P, N_POS], F32)
-        nc.gpsimd.tensor_scalar(
-            out=minus_angle[:], in0=pos[:], scalar1=-2.0 * math.pi, scalar2=0.0, op0=ALU.mult, op1=ALU.add
-        )
+        frac_of[0] = add_tail(0, turns_of[0])
 
         w_emb = keep.tile([P, D], BF16)
         for g in range(PASSES):
@@ -222,39 +257,17 @@ def tile_ffnn_encoder_pa_t_kernel(
 
         timing = keep.tile([P, N_POS, 2, PACK, P], F32)
 
-        def make_turns(a):
-            fast = fast_quads(a)
-            here = pos[:, a : a + 1]
-            shape = [P, PACK, fast]
-            turns = work.tile(shape, F32, bufs=2)
-            nc.vector.tensor_scalar(
-                out=turns[:], in0=f_head[:, :, 0:fast], scalar1=here, scalar2=-0.125,
-                op0=ALU.mult, op1=ALU.add,
-            )
-            whole = work.tile(shape, F32, bufs=2)
-            nc.vector.tensor_scalar(
-                out=whole[:], in0=turns[:], scalar1=ROUND_TO_INT, scalar2=ROUND_TO_INT,
-                op0=ALU.add, op1=ALU.subtract,
-            )
-            nc.vector.tensor_tensor(out=whole[:], in0=turns[:], in1=whole[:], op=ALU.subtract)
-            frac = work.tile(shape, F32, bufs=4)
-            nc.vector.scalar_tensor_tensor(
-                out=frac[:], in0=f_tail[:, :, 0:fast], scalar=here, in1=whole[:],
-                op0=ALU.mult, op1=ALU.add,
-            )
-            return frac
-
         def fast_signal(a, frac):
             fast = fast_quads(a)
-            distance = work.tile([P, 2, PACK, fast], F32, bufs=2)
             for half, shift in enumerate((minus_eighth, plus_eighth)):
+                distance = work.tile([P, PACK, fast], F32, bufs=3)
                 nc.scalar.activation(
-                    out=distance[:, half], in_=frac[:], func=FUNC.Abs, bias=shift[:], scale=1.0
+                    out=distance[:], in_=frac[:], func=FUNC.Abs, bias=shift[:], scale=1.0
                 )
-            nc.scalar.activation(
-                out=timing[:, a, :, :, 0:fast], in_=distance[:], func=FUNC.Sin,
-                bias=quarter_turn[:], scale=-2.0 * math.pi,
-            )
+                nc.scalar.activation(
+                    out=timing[:, a, half, :, 0:fast], in_=distance[:], func=FUNC.Sin,
+                    bias=quarter_turn[:], scale=-2.0 * math.pi,
+                )
 
         def slow_signal(a):
             fast = fast_quads(a)
@@ -308,36 +321,35 @@ def tile_ffnn_encoder_pa_t_kernel(
                 accum_out=sum_e[:, b, half : half + 1],
             )
 
-        def sum_of_squares(e, b, sum_sq):
+        def mean_of_squares(e, b, mean_sq):
             squares = work.tile([P, D], BF16, bufs=2)
             nc.scalar.activation(
-                out=squares[:], in_=e[:], func=FUNC.Square, accum_out=sum_sq[:, b : b + 1]
+                out=squares[:], in_=e[:], func=FUNC.Square, scale=1.0 / ROOT_D,
+                accum_out=mean_sq[:, b : b + 1],
             )
 
-        def statistics(sum_e, sum_sq):
+        def statistics(sum_e, mean_sq):
             total = work.tile([P, BATCH], F32, bufs=2)
             nc.gpsimd.tensor_tensor(out=total[:], in0=sum_e[:, :, 0], in1=sum_e[:, :, 1], op=ALU.add)
             minus_mean = work.tile([P, BATCH], F32, bufs=2)
             nc.gpsimd.tensor_scalar(
                 out=minus_mean[:], in0=total[:], scalar1=-1.0 / D, scalar2=0.0, op0=ALU.mult, op1=ALU.add
             )
-            mean_sq = work.tile([P, BATCH], F32, bufs=2)
-            nc.gpsimd.tensor_tensor(out=mean_sq[:], in0=minus_mean[:], in1=minus_mean[:], op=ALU.mult)
-            var_eps = work.tile([P, BATCH], F32, bufs=2)
+            less_eps = work.tile([P, BATCH], F32, bufs=2)
+            nc.gpsimd.tensor_tensor(out=less_eps[:], in0=minus_mean[:], in1=minus_mean[:], op=ALU.mult)
             nc.gpsimd.tensor_scalar(
-                out=var_eps[:], in0=sum_sq[:], scalar1=1.0 / D, scalar2=EPS, op0=ALU.mult, op1=ALU.add
+                out=less_eps[:], in0=less_eps[:], scalar1=1.0, scalar2=-EPS, op0=ALU.mult, op1=ALU.add
             )
-            nc.gpsimd.tensor_tensor(out=var_eps[:], in0=var_eps[:], in1=mean_sq[:], op=ALU.subtract)
+            var_eps = work.tile([P, BATCH], F32, bufs=2)
+            nc.gpsimd.tensor_tensor(out=var_eps[:], in0=mean_sq[:], in1=less_eps[:], op=ALU.subtract)
             rstd = work.tile([P, BATCH], F32, bufs=2)
             nc.gpsimd.tensor_tensor(out=rstd[:], in0=var_eps[:], in1=minus_half[:], op=ALU.pow)
-            shift = work.tile([P, BATCH], F32, bufs=2)
-            nc.gpsimd.tensor_tensor(out=shift[:], in0=minus_mean[:], in1=rstd[:], op=ALU.mult)
-            return rstd, shift
+            return minus_mean, rstd
 
-        def normalise(engine, b, e, rstd, shift):
+        def normalise(engine, b, e, minus_mean, rstd):
             engine.tensor_scalar(
-                out=e[:], in0=e[:], scalar1=rstd[:, b : b + 1],
-                scalar2=shift[:, b : b + 1], op0=ALU.mult, op1=ALU.add,
+                out=e[:], in0=e[:], scalar1=minus_mean[:, b : b + 1],
+                scalar2=rstd[:, b : b + 1], op0=ALU.add, op1=ALU.mult,
             )
 
         def scale_and_shift(normed_tiles, c, planes):
@@ -421,9 +433,10 @@ def tile_ffnn_encoder_pa_t_kernel(
         x_t_of = {0: transpose_x(0)}
         z_of_tile = [embed_bank(0, half, x_t_of[0]) for half in range(HALVES)]
         slow_signal(0)
-        fast_signal(0, make_turns(0))
+        fast_signal(0, frac_of[0])
         x_t_of[1] = transpose_x(1)
-        frac_of = {1: make_turns(1), 2: make_turns(2)}
+        for a in (1, 2):
+            frac_of[a] = add_tail(a, make_turns(a))
         nc.gpsimd.tensor_copy(
             out=cols[:].rearrange("p (v c) -> p v c", v=3), in_=vectors[:, :, 0:CHUNKS]
         )
@@ -439,8 +452,8 @@ def tile_ffnn_encoder_pa_t_kernel(
             if group is not None:
                 if b == 0:
                     sum_e = work.tile([P, BATCH, HALVES], F32, bufs=3)
-                    sum_sq = work.tile([P, BATCH], F32, bufs=3)
-                    sums_of[group] = (sum_e, sum_sq)
+                    mean_sq = work.tile([P, BATCH], F32, bufs=3)
+                    sums_of[group] = (sum_e, mean_sq)
                     e_of[group] = []
                 e = work.tile([P, D], F32, bufs=16)
                 e_of[group].append(e)
@@ -478,7 +491,15 @@ def tile_ffnn_encoder_pa_t_kernel(
                 if of_b == 0:
                     result = work.tile([P, BATCH, N_ALL], F32, bufs=2)
                 add_bias(of_b, acc_qk, acc_v_of, result)
-                if of_b == BATCH - 1:
+                if of_group == N_POS - 1:
+                    for w, out in enumerate((out_0, out_1, out_2)):
+                        if w < 2 or of_b % 2 == 1:
+                            first = of_b if w < 2 else of_b - 1
+                            nc.sync.dma_start(
+                                out=out.rearrange("b (a p) n -> a p b n", p=P)[of_group][:, first : of_b + 1],
+                                in_=result[:, first : of_b + 1, w * N_OUT : (w + 1) * N_OUT],
+                            )
+                elif of_b == BATCH - 1:
                     for w, out in enumerate((out_0, out_1, out_2)):
                         nc.sync.dma_start(
                             out=out.rearrange("b (a p) n -> a p b n", p=P)[of_group],
@@ -494,7 +515,7 @@ def tile_ffnn_encoder_pa_t_kernel(
                     h_mx_of[quantised] = []
                 h_mx_of[quantised].append(quantise(grouped))
             if group is not None:
-                sum_of_squares(e, b, sums_of[group][1])
+                mean_of_squares(e, b, sums_of[group][1])
 
             w = step - WEIGHTS_AT
             if 0 <= w < 3:
@@ -511,7 +532,7 @@ def tile_ffnn_encoder_pa_t_kernel(
             if signalled < N_POS:
                 slow_signal(signalled)
             if signalled + 2 < N_POS:
-                frac_of[signalled + 2] = make_turns(signalled + 2)
+                frac_of[signalled + 2] = add_tail(signalled + 2, make_turns(signalled + 2))
             ready, tile_b = group_at(step, PROJECT_AT)
             if ready is not None:
                 if tile_b % 2 == 0:

@@ -180,34 +180,37 @@ def tile_ffnn_encoder_pa_t_kernel(
         nc.vector.tensor_single_scalar(
             out=f_head[:].bitcast(I32), in_=product[:].bitcast(I32), scalar=-2048, op=ALU.bitwise_and
         )
-        def make_turns(a):
-            fast = fast_quads(a)
-            here = pos[:, a : a + 1]
-            shape = [P, PACK, fast]
-            turns = work.tile(shape, F32, bufs=2)
-            nc.vector.tensor_scalar(
-                out=turns[:], in0=f_head[:, :, 0:fast], scalar1=here, scalar2=-0.125,
-                op0=ALU.mult, op1=ALU.add,
-            )
-            whole = work.tile(shape, F32, bufs=2)
-            nc.vector.tensor_scalar(
-                out=whole[:], in0=turns[:], scalar1=ROUND_TO_INT, scalar2=ROUND_TO_INT,
-                op0=ALU.add, op1=ALU.subtract,
-            )
-            nc.vector.tensor_tensor(out=whole[:], in0=turns[:], in1=whole[:], op=ALU.subtract)
-            return whole
+        def make_turns(tiles):
+            turns_of = {}
+            whole_of = {}
+            for a in tiles:
+                turns_of[a] = work.tile([P, PACK, fast_quads(a)], F32, name="turns", bufs=3)
+                nc.vector.tensor_scalar(
+                    out=turns_of[a][:], in0=f_head[:, :, 0 : fast_quads(a)],
+                    scalar1=pos[:, a : a + 1], scalar2=-0.125, op0=ALU.mult, op1=ALU.add,
+                )
+            for a in tiles:
+                whole_of[a] = work.tile([P, PACK, fast_quads(a)], F32, name="whole", bufs=3)
+                nc.vector.tensor_scalar(
+                    out=whole_of[a][:], in0=turns_of[a][:], scalar1=ROUND_TO_INT,
+                    scalar2=ROUND_TO_INT, op0=ALU.add, op1=ALU.subtract,
+                )
+            for a in tiles:
+                nc.vector.tensor_tensor(
+                    out=whole_of[a][:], in0=turns_of[a][:], in1=whole_of[a][:], op=ALU.subtract
+                )
+            return whole_of
 
-        def add_tail(a, whole):
-            fast = fast_quads(a)
-            frac = work.tile([P, PACK, fast], F32, bufs=4)
-            nc.vector.scalar_tensor_tensor(
-                out=frac[:], in0=f_tail[:, :, 0:fast], scalar=pos[:, a : a + 1], in1=whole[:],
-                op0=ALU.mult, op1=ALU.add,
-            )
-            return frac
+        def add_tails(whole_of):
+            for a, whole in whole_of.items():
+                frac_of[a] = work.tile([P, PACK, fast_quads(a)], F32, name="frac", bufs=5)
+                nc.vector.scalar_tensor_tensor(
+                    out=frac_of[a][:], in0=f_tail[:, :, 0 : fast_quads(a)],
+                    scalar=pos[:, a : a + 1], in1=whole[:], op0=ALU.mult, op1=ALU.add,
+                )
 
         frac_of = {}
-        turns_of = {0: make_turns(0)}
+        first_turns = make_turns((0,))
         nc.vector.tensor_tensor(out=coarse_all[:], in0=coarse_hd[:], in1=coarse_tl[:], op=ALU.add)
         nc.vector.tensor_tensor(out=fine_all[:], in0=fine_hd[:], in1=fine_tl[:], op=ALU.add)
         nc.vector.tensor_tensor(
@@ -225,7 +228,8 @@ def tile_ffnn_encoder_pa_t_kernel(
         )
         nc.vector.tensor_tensor(out=cross[:], in0=product[:], in1=cross[:], op=ALU.add)
         nc.vector.tensor_tensor(out=f_tail[:], in0=cross[:], in1=cross2[:], op=ALU.add)
-        frac_of[0] = add_tail(0, turns_of[0])
+        add_tails(first_turns)
+        add_tails(make_turns((1, 2)))
 
         w_emb = keep.tile([P, D], BF16)
         for g in range(PASSES):
@@ -286,7 +290,7 @@ def tile_ffnn_encoder_pa_t_kernel(
                 nc.tensor.transpose(
                     out=x_t_ps[:, b * P : (b + 1) * P], in_=x_sb[:, a, b, :], identity=ident_b[:]
                 )
-            x_t = work.tile([P, GROUP], BF16, bufs=2)
+            x_t = work.tile([P, GROUP], BF16, bufs=3)
             nc.scalar.copy(out=x_t[:], in_=x_t_ps[:])
             return x_t
 
@@ -416,18 +420,37 @@ def tile_ffnn_encoder_pa_t_kernel(
                     op=ALU.add,
                 )
 
+        def store_tile(group, b, result):
+            for w, out in enumerate((out_0, out_1, out_2)):
+                first = b if w < 2 else b - 1
+                if w < 2 or b % 2 == 1:
+                    nc.sync.dma_start(
+                        out=out.rearrange("b (a p) n -> a p b n", p=P)[group][:, first : b + 1],
+                        in_=result[:, first : b + 1, w * N_OUT : (w + 1) * N_OUT],
+                    )
+
+        def store_group(group, result):
+            for w, out in enumerate((out_0, out_1, out_2)):
+                nc.sync.dma_start(
+                    out=out.rearrange("b (a p) n -> a p b n", p=P)[group],
+                    in_=result[:, :, w * N_OUT : (w + 1) * N_OUT],
+                )
+
         STATS_AT = 5
         NORM_AT = 6
-        TURN_AT = 8
+        TURN_AT = 7
+        REGROUP_AT = 11
         QUANT_AT = 12
-        PROJECT_AT = 16
+        PROJECT_AT = 13
         CHUNKS_A_STEP = CHUNKS // BATCH
-        WEIGHTS_AT = 6
-        WEIGHT_LAG = 2
 
         def group_at(step, lag):
             group, place = divmod(step - lag, BATCH)
             return (group if 0 <= group < N_POS else None), place
+
+        signal_at = {(3 if a < 4 else BATCH) * (a - 1): a for a in range(1, N_POS)}
+        regroup_weight_at = {2 * w + 2: w for w in range(3)}
+        quantise_weight_at = {2 * w + 4: w for w in range(3)}
 
         cols = keep.tile([P, 3 * CHUNKS], F32)
         x_t_of = {0: transpose_x(0)}
@@ -435,8 +458,6 @@ def tile_ffnn_encoder_pa_t_kernel(
         slow_signal(0)
         fast_signal(0, frac_of[0])
         x_t_of[1] = transpose_x(1)
-        for a in (1, 2):
-            frac_of[a] = add_tail(a, make_turns(a))
         nc.gpsimd.tensor_copy(
             out=cols[:].rearrange("p (v c) -> p v c", v=3), in_=vectors[:, :, 0:CHUNKS]
         )
@@ -444,6 +465,7 @@ def tile_ffnn_encoder_pa_t_kernel(
         e_of = {}
         stats_of = {}
         planes_of = {}
+        grouped_of = {}
         h_mx_of = {}
         w_grouped_of = {}
         projected = None
@@ -462,81 +484,64 @@ def tile_ffnn_encoder_pa_t_kernel(
 
             done, place = group_at(step, STATS_AT)
             if done is not None and place == 0:
-                stats_of[done] = statistics(sums_of[done][0], sums_of[done][1])
+                stats_of[done] = statistics(*sums_of[done])
                 for tile_b in (2, 3):
                     normalise(nc.gpsimd, tile_b, e_of[done][tile_b], *stats_of[done])
 
-            grouped = None
+            regrouped, g = group_at(step, REGROUP_AT)
+            if regrouped is not None and g < PASSES:
+                grouped_of[regrouped, g] = regroup(planes_of[regrouped, g])
             quantised, place = group_at(step, QUANT_AT)
-            g, odd = divmod(place, 2)
-            if quantised is not None and odd == 0:
-                grouped = regroup(planes_of[quantised][g])
+            if quantised is not None and place == 0:
+                h_mx_of[quantised] = [quantise(grouped_of[quantised, g]) for g in range(PASSES)]
             done, place = group_at(step, NORM_AT)
             if done is not None and place == 0:
                 for tile_b in (0, 1):
                     normalise(nc.vector, tile_b, e_of[done][tile_b], *stats_of[done])
-
-            turned, j = group_at(step, TURN_AT)
-            if turned is not None:
-                c = j * CHUNKS_A_STEP
-                if c == 0:
-                    planes_of[turned] = []
-                if c % PACK == 0:
-                    planes = work.tile([P, PACK // 2, GROUP, 2], BF16, bufs=4)
-                    planes_of[turned].append(planes)
-                scale_and_shift(e_of[turned], c, planes)
-
             if projected is not None:
                 of_group, of_b, acc_qk, acc_v_of = projected
                 if of_b == 0:
                     result = work.tile([P, BATCH, N_ALL], F32, bufs=2)
                 add_bias(of_b, acc_qk, acc_v_of, result)
                 if of_group == N_POS - 1:
-                    for w, out in enumerate((out_0, out_1, out_2)):
-                        if w < 2 or of_b % 2 == 1:
-                            first = of_b if w < 2 else of_b - 1
-                            nc.sync.dma_start(
-                                out=out.rearrange("b (a p) n -> a p b n", p=P)[of_group][:, first : of_b + 1],
-                                in_=result[:, first : of_b + 1, w * N_OUT : (w + 1) * N_OUT],
-                            )
+                    store_tile(of_group, of_b, result)
                 elif of_b == BATCH - 1:
-                    for w, out in enumerate((out_0, out_1, out_2)):
-                        nc.sync.dma_start(
-                            out=out.rearrange("b (a p) n -> a p b n", p=P)[of_group],
-                            in_=result[:, :, w * N_OUT : (w + 1) * N_OUT],
-                        )
+                    store_group(of_group, result)
                 projected = None
 
-            signalled = step + 1
-            if signalled < N_POS:
+            signalled = signal_at.get(step)
+            if signalled is not None:
                 fast_signal(signalled, frac_of[signalled])
-            if grouped is not None:
-                if g == 0:
-                    h_mx_of[quantised] = []
-                h_mx_of[quantised].append(quantise(grouped))
+            turned, j = group_at(step, TURN_AT)
+            c = j * CHUNKS_A_STEP
+            if turned is not None:
+                if c % PACK == 0:
+                    planes_of[turned, c // PACK] = work.tile(
+                        [P, PACK // 2, GROUP, 2], BF16, name="planes", bufs=4
+                    )
+                scale_and_shift(e_of[turned], c, planes_of[turned, c // PACK])
             if group is not None:
                 mean_of_squares(e, b, sums_of[group][1])
-
-            w = step - WEIGHTS_AT
-            if 0 <= w < 3:
-                w_grouped_of[w] = regroup_weight(w)
-            w = step - WEIGHTS_AT - WEIGHT_LAG
-            if 0 <= w < 3:
-                quantise_weight(w, w_grouped_of[w])
-
+            if signalled is not None:
+                slow_signal(signalled)
+            pair, place = divmod(step, 2 * BATCH)
+            if place == 3 and 2 * pair + 3 < N_POS:
+                add_tails(make_turns(range(2 * pair + 3, min(2 * pair + 5, N_POS))))
             following, next_b = group_at(step + 1, 0)
             if following is not None:
                 z_of_tile = [embed_bank(next_b, half, x_t_of[following]) for half in range(HALVES)]
             if turned is not None:
-                scale_and_shift(e_of[turned], c + 1, planes)
-            if signalled < N_POS:
-                slow_signal(signalled)
-            if signalled + 2 < N_POS:
-                frac_of[signalled + 2] = add_tail(signalled + 2, make_turns(signalled + 2))
+                scale_and_shift(e_of[turned], c + 1, planes_of[turned, c // PACK])
             ready, tile_b = group_at(step, PROJECT_AT)
             if ready is not None:
                 if tile_b % 2 == 0:
                     acc_v = psum_o.tile([P, 2, N_OUT], F32, bufs=1)
                 projected = (ready, tile_b, project(tile_b, h_mx_of[ready], acc_v), acc_v)
-            if group is not None and b == 2 and group + 2 < N_POS:
+            w = regroup_weight_at.get(step)
+            if w is not None:
+                w_grouped_of[w] = regroup_weight(w)
+            w = quantise_weight_at.get(step)
+            if w is not None:
+                quantise_weight(w, w_grouped_of[w])
+            if group is not None and b == 1 and group + 2 < N_POS:
                 x_t_of[group + 2] = transpose_x(group + 2)

@@ -356,7 +356,7 @@ def tile_ffnn_encoder_pa_t_kernel(
                 scalar2=rstd[:, b : b + 1], op0=ALU.add, op1=ALU.mult,
             )
 
-        def scale_and_shift(normed_tiles, c, planes):
+        def scale_and_shift(normed_tiles, c, half):
             normed_t = psum_t.tile([P, GROUP], F32, tag="tp")
             for b in range(BATCH):
                 nc.tensor.transpose(
@@ -365,19 +365,35 @@ def tile_ffnn_encoder_pa_t_kernel(
                     identity=ident_f[:],
                 )
             nc.scalar.activation(
-                out=planes[:, c % PACK // 2, :, c % 2], in_=normed_t[:], func=FUNC.Identity,
+                out=half, in_=normed_t[:], func=FUNC.Identity,
                 scale=cols[:, CHUNKS + c : CHUNKS + c + 1],
                 bias=cols[:, 2 * CHUNKS + c : 2 * CHUNKS + c + 1],
             )
 
-        def regroup(planes):
+        def is_paired(group, g):
+            return not (g == 1)
+
+        def new_planes(group, g):
+            shape = [P, PACK // 2, GROUP, 2] if is_paired(group, g) else [P, PACK, GROUP]
+            return work.tile(shape, BF16, name="planes", tag="planes", bufs=4)
+
+        def value_of(planes, group, g, t):
+            return planes[:, t // 2, :, t % 2] if is_paired(group, g) else planes[:, t, :]
+
+        def regroup(planes, group, g):
             grouped = work.tile([P, GROUP, PACK], BF16, bufs=2, align_bytes=64)
-            nc.vector.tensor_copy(
-                out=grouped[:].rearrange("p r t -> p (r t)").bitcast(F32)
-                .rearrange("p (r u) -> p r u", u=PACK // 2),
-                in_=planes[:].rearrange("p u r e -> p (u r e)").bitcast(F32)
-                .rearrange("p (u r) -> p r u", u=PACK // 2),
-            )
+            if is_paired(group, g):
+                nc.vector.tensor_copy(
+                    out=grouped[:].rearrange("p r t -> p (r t)").bitcast(F32)
+                    .rearrange("p (r u) -> p r u", u=PACK // 2),
+                    in_=planes[:].rearrange("p u r e -> p (u r e)").bitcast(F32)
+                    .rearrange("p (u r) -> p r u", u=PACK // 2),
+                )
+            else:
+                nc.vector.tensor_copy(
+                    out=grouped[:].rearrange("p (k i) t -> p k t i", i=4),
+                    in_=planes[:].rearrange("p t (k i) -> p k t i", i=4),
+                )
             return grouped
 
         def quantise(grouped):
@@ -490,7 +506,7 @@ def tile_ffnn_encoder_pa_t_kernel(
 
             regrouped, g = group_at(step, REGROUP_AT)
             if regrouped is not None and g < PASSES:
-                grouped_of[regrouped, g] = regroup(planes_of[regrouped, g])
+                grouped_of[regrouped, g] = regroup(planes_of[regrouped, g], regrouped, g)
             quantised, place = group_at(step, QUANT_AT)
             if quantised is not None and place == 0:
                 h_mx_of[quantised] = [quantise(grouped_of[quantised, g]) for g in range(PASSES)]
@@ -515,11 +531,11 @@ def tile_ffnn_encoder_pa_t_kernel(
             turned, j = group_at(step, TURN_AT)
             c = j * CHUNKS_A_STEP
             if turned is not None:
-                if c % PACK == 0:
-                    planes_of[turned, c // PACK] = work.tile(
-                        [P, PACK // 2, GROUP, 2], BF16, name="planes", bufs=4
-                    )
-                scale_and_shift(e_of[turned], c, planes_of[turned, c // PACK])
+                g_turned, t = divmod(c, PACK)
+                if t == 0:
+                    planes_of[turned, g_turned] = new_planes(turned, g_turned)
+                planes = planes_of[turned, g_turned]
+                scale_and_shift(e_of[turned], c, value_of(planes, turned, g_turned, t))
             if group is not None:
                 mean_of_squares(e, b, sums_of[group][1])
             if signalled is not None:
@@ -531,7 +547,7 @@ def tile_ffnn_encoder_pa_t_kernel(
             if following is not None:
                 z_of_tile = [embed_bank(next_b, half, x_t_of[following]) for half in range(HALVES)]
             if turned is not None:
-                scale_and_shift(e_of[turned], c + 1, planes_of[turned, c // PACK])
+                scale_and_shift(e_of[turned], c + 1, value_of(planes, turned, g_turned, t + 1))
             ready, tile_b = group_at(step, PROJECT_AT)
             if ready is not None:
                 if tile_b % 2 == 0:

@@ -102,8 +102,6 @@ def tile_ffnn_encoder_pa_t_kernel(
 
         one = keep.tile([P, 1], F32)
         nc.vector.memset(one[:], 1.0)
-        warm = keep.tile([P, 1], F32)
-        nc.scalar.activation(out=warm[:], in_=one[:], func=FUNC.Sin)
         quarter_turn = keep.tile([P, 1], F32)
         nc.scalar.mul(out=quarter_turn[:], in_=one[:], mul=0.5 * math.pi)
         ident_b = keep.tile([P, P], BF16)
@@ -126,6 +124,8 @@ def tile_ffnn_encoder_pa_t_kernel(
             else:
                 nc.gpsimd.memset(head, head_of(value))
                 nc.scalar.mul(out=tail, in_=one[:], mul=value - head_of(value))
+        warm = keep.tile([P, 1], F32)
+        nc.scalar.activation(out=warm[:], in_=one[:], func=FUNC.Sin)
         pos = keep.tile([P, N_POS], F32)
         nc.gpsimd.iota(
             out=pos[:], pattern=[[P, N_POS]], base=0, channel_multiplier=1,
@@ -173,63 +173,69 @@ def tile_ffnn_encoder_pa_t_kernel(
         f_slow = keep.tile([P, PACK, (COARSE - SLOW_FROM) * QUADS], F32)
         fine_all = keep.tile([P, FINE], F32)
         coarse_all = keep.tile([P, COARSE], F32)
+        turns_of = {}
+        whole_of = {}
+        frac_of = {}
+
+        def to_turns(a):
+            turns_of[a] = work.tile([P, PACK, fast_quads(a)], F32, name="turns", bufs=3)
+            nc.vector.tensor_scalar(
+                out=turns_of[a][:], in0=f_head[:, :, 0 : fast_quads(a)],
+                scalar1=pos[:, a : a + 1], scalar2=-0.125, op0=ALU.mult, op1=ALU.add,
+            )
+
+        def to_whole(a):
+            whole_of[a] = work.tile([P, PACK, fast_quads(a)], F32, name="whole", bufs=3)
+            nc.vector.tensor_scalar(
+                out=whole_of[a][:], in0=turns_of[a][:], scalar1=ROUND_TO_INT,
+                scalar2=ROUND_TO_INT, op0=ALU.add, op1=ALU.subtract,
+            )
+
+        def less_whole(a):
+            nc.vector.tensor_tensor(
+                out=whole_of[a][:], in0=turns_of[a][:], in1=whole_of[a][:], op=ALU.subtract
+            )
+
+        def add_tail(a):
+            frac_of[a] = work.tile([P, PACK, fast_quads(a)], F32, name="frac", bufs=5)
+            nc.vector.scalar_tensor_tensor(
+                out=frac_of[a][:], in0=f_tail[:, :, 0 : fast_quads(a)],
+                scalar=pos[:, a : a + 1], in1=whole_of[a][:], op0=ALU.mult, op1=ALU.add,
+            )
+
         nc.vector.tensor_tensor(
             out=as_grid(product), in0=over_fine(coarse_hd, 0, FAST_COARSE),
             in1=over_coarse(fine_hd, FAST_COARSE), op=ALU.mult,
         )
+        nc.vector.tensor_tensor(out=coarse_all[:], in0=coarse_hd[:], in1=coarse_tl[:], op=ALU.add)
         nc.vector.tensor_single_scalar(
             out=f_head[:].bitcast(I32), in_=product[:].bitcast(I32), scalar=-2048, op=ALU.bitwise_and
         )
-        def make_turns(tiles):
-            turns_of = {}
-            whole_of = {}
-            for a in tiles:
-                turns_of[a] = work.tile([P, PACK, fast_quads(a)], F32, name="turns", bufs=3)
-                nc.vector.tensor_scalar(
-                    out=turns_of[a][:], in0=f_head[:, :, 0 : fast_quads(a)],
-                    scalar1=pos[:, a : a + 1], scalar2=-0.125, op0=ALU.mult, op1=ALU.add,
-                )
-            for a in tiles:
-                whole_of[a] = work.tile([P, PACK, fast_quads(a)], F32, name="whole", bufs=3)
-                nc.vector.tensor_scalar(
-                    out=whole_of[a][:], in0=turns_of[a][:], scalar1=ROUND_TO_INT,
-                    scalar2=ROUND_TO_INT, op0=ALU.add, op1=ALU.subtract,
-                )
-            for a in tiles:
-                nc.vector.tensor_tensor(
-                    out=whole_of[a][:], in0=turns_of[a][:], in1=whole_of[a][:], op=ALU.subtract
-                )
-            return whole_of
-
-        def add_tails(whole_of):
-            for a, whole in whole_of.items():
-                frac_of[a] = work.tile([P, PACK, fast_quads(a)], F32, name="frac", bufs=5)
-                nc.vector.scalar_tensor_tensor(
-                    out=frac_of[a][:], in0=f_tail[:, :, 0 : fast_quads(a)],
-                    scalar=pos[:, a : a + 1], in1=whole[:], op0=ALU.mult, op1=ALU.add,
-                )
-
-        frac_of = {}
-        first_turns = make_turns((0,))
-        nc.vector.tensor_tensor(out=coarse_all[:], in0=coarse_hd[:], in1=coarse_tl[:], op=ALU.add)
         nc.vector.tensor_tensor(out=fine_all[:], in0=fine_hd[:], in1=fine_tl[:], op=ALU.add)
-        nc.vector.tensor_tensor(
-            out=as_grid(f_slow), in0=over_fine(coarse_all, SLOW_FROM, COARSE),
-            in1=over_coarse(fine_all, COARSE - SLOW_FROM), op=ALU.mult,
-        )
         nc.vector.tensor_tensor(
             out=as_grid(cross), in0=over_fine(coarse_hd, 0, FAST_COARSE),
             in1=over_coarse(fine_tl, FAST_COARSE), op=ALU.mult,
         )
+        to_turns(0)
         nc.vector.tensor_tensor(out=product[:], in0=product[:], in1=f_head[:], op=ALU.subtract)
+        nc.vector.tensor_tensor(
+            out=as_grid(f_slow), in0=over_fine(coarse_all, SLOW_FROM, COARSE),
+            in1=over_coarse(fine_all, COARSE - SLOW_FROM), op=ALU.mult,
+        )
+        to_whole(0)
+        nc.vector.tensor_tensor(out=cross[:], in0=product[:], in1=cross[:], op=ALU.add)
         nc.vector.tensor_tensor(
             out=as_grid(cross2), in0=over_fine(coarse_tl, 0, FAST_COARSE),
             in1=over_coarse(fine_all, FAST_COARSE), op=ALU.mult,
         )
-        nc.vector.tensor_tensor(out=cross[:], in0=product[:], in1=cross[:], op=ALU.add)
+        less_whole(0)
         nc.vector.tensor_tensor(out=f_tail[:], in0=cross[:], in1=cross2[:], op=ALU.add)
-        add_tails(first_turns)
-        add_tails(make_turns((1, 2)))
+        to_turns(1)
+        to_turns(2)
+        add_tail(0)
+        for stage in (to_whole, less_whole, add_tail):
+            for a in (1, 2):
+                stage(a)
 
         w_emb = keep.tile([P, D], BF16)
         for g in range(PASSES):
@@ -351,10 +357,13 @@ def tile_ffnn_encoder_pa_t_kernel(
             return minus_mean, rstd
 
         def normalise(engine, b, e, minus_mean, rstd):
-            engine.tensor_scalar(
-                out=e[:], in0=e[:], scalar1=minus_mean[:, b : b + 1],
-                scalar2=rstd[:, b : b + 1], op0=ALU.add, op1=ALU.mult,
-            )
+            width = D // 2 if engine is nc.gpsimd else D
+            for first in range(0, D, width):
+                part = e[:, first : first + width]
+                engine.tensor_scalar(
+                    out=part, in0=part, scalar1=minus_mean[:, b : b + 1],
+                    scalar2=rstd[:, b : b + 1], op0=ALU.add, op1=ALU.mult,
+                )
 
         def scale_and_shift(normed_tiles, c, half):
             normed_t = psum_t.tile([P, GROUP], F32, tag="tp")
@@ -508,8 +517,11 @@ def tile_ffnn_encoder_pa_t_kernel(
             if regrouped is not None and g < PASSES:
                 grouped_of[regrouped, g] = regroup(planes_of[regrouped, g], regrouped, g)
             quantised, place = group_at(step, QUANT_AT)
+            if regrouped is not None and regrouped == N_POS - 1 and g == 0:
+                h_mx_of[regrouped] = [quantise(grouped_of[regrouped, 0])]
             if quantised is not None and place == 0:
-                h_mx_of[quantised] = [quantise(grouped_of[quantised, g]) for g in range(PASSES)]
+                first = len(h_mx_of.setdefault(quantised, []))
+                h_mx_of[quantised] += [quantise(grouped_of[quantised, g]) for g in range(first, PASSES)]
             done, place = group_at(step, NORM_AT)
             if done is not None and place == 0:
                 for tile_b in (0, 1):
@@ -542,7 +554,9 @@ def tile_ffnn_encoder_pa_t_kernel(
                 slow_signal(signalled)
             pair, place = divmod(step, 2 * BATCH)
             if place == 3 and 2 * pair + 3 < N_POS:
-                add_tails(make_turns(range(2 * pair + 3, min(2 * pair + 5, N_POS))))
+                for stage in (to_turns, to_whole, less_whole, add_tail):
+                    for a in range(2 * pair + 3, min(2 * pair + 5, N_POS)):
+                        stage(a)
             following, next_b = group_at(step + 1, 0)
             if following is not None:
                 z_of_tile = [embed_bank(next_b, half, x_t_of[following]) for half in range(HALVES)]

@@ -249,7 +249,7 @@ def tile_ffnn_encoder_pa_t_kernel(
         w_scales = keep.tile([P, PASSES, N_ALL], U8, align_bytes=64)
 
         def regroup_weight(w):
-            w_grouped = work.tile([P, PASSES, N_OUT, PACK], BF16, bufs=2, align_bytes=64)
+            w_grouped = work.tile([P, PASSES, N_OUT, PACK], BF16, bufs=3, align_bytes=64)
             src = w_raw[w][:].rearrange("p g t n -> p g n t")
             nc.gpsimd.tensor_scalar(
                 out=w_grouped[:], in0=src, scalar1=1.0, scalar2=0.0, op0=ALU.mult, op1=ALU.add
@@ -464,7 +464,7 @@ def tile_ffnn_encoder_pa_t_kernel(
         STATS_AT = 5
         NORM_AT = 6
         TURN_AT = 7
-        REGROUP_AT = 11
+        REGROUP_AT = 10
         QUANT_AT = 12
         PROJECT_AT = 13
         CHUNKS_A_STEP = CHUNKS // BATCH
@@ -473,9 +473,10 @@ def tile_ffnn_encoder_pa_t_kernel(
             group, place = divmod(step - lag, BATCH)
             return (group if 0 <= group < N_POS else None), place
 
-        signal_at = {(3 if a < 4 else BATCH) * (a - 1): a for a in range(1, N_POS)}
-        regroup_weight_at = {2 * w + 2: w for w in range(3)}
-        quantise_weight_at = {2 * w + 4: w for w in range(3)}
+        signal_at = {(3 * (a - 1) if a < 4 else BATCH * a - 2): a for a in range(1, N_POS)}
+        turns_at = {4: (3, 4), 11: (5, 6), 19: (7,)}
+        regroup_weight_at = {1 + w: w for w in range(3)}
+        quantise_weight_at = {7 + w: w for w in range(3)}
 
         cols = keep.tile([P, 3 * CHUNKS], F32)
         x_t_of = {0: transpose_x(0)}
@@ -502,7 +503,7 @@ def tile_ffnn_encoder_pa_t_kernel(
                     mean_sq = work.tile([P, BATCH], F32, bufs=3)
                     sums_of[group] = (sum_e, mean_sq)
                     e_of[group] = []
-                e = work.tile([P, D], F32, bufs=16)
+                e = work.tile([P, D], F32, bufs=14)
                 e_of[group].append(e)
                 for half in range(HALVES):
                     add_timing(group, b, half, z_of_tile[half], e, sums_of[group][0])
@@ -513,15 +514,19 @@ def tile_ffnn_encoder_pa_t_kernel(
                 for tile_b in (2, 3):
                     normalise(nc.gpsimd, tile_b, e_of[done][tile_b], *stats_of[done])
 
-            regrouped, g = group_at(step, REGROUP_AT)
-            if regrouped is not None and g < PASSES:
+            regrouped, place = group_at(step, REGROUP_AT)
+            g, odd = divmod(place, 2)
+            if regrouped is not None and odd == 0:
                 grouped_of[regrouped, g] = regroup(planes_of[regrouped, g], regrouped, g)
             quantised, place = group_at(step, QUANT_AT)
-            if regrouped is not None and regrouped == N_POS - 1 and g == 0:
-                h_mx_of[regrouped] = [quantise(grouped_of[regrouped, 0])]
-            if quantised is not None and place == 0:
-                first = len(h_mx_of.setdefault(quantised, []))
-                h_mx_of[quantised] += [quantise(grouped_of[quantised, g]) for g in range(first, PASSES)]
+            if regrouped == N_POS - 1 and odd == 0:
+                ready_passes = ((regrouped, g),)
+            elif quantised is not None and quantised < N_POS - 1 and place == 0:
+                ready_passes = tuple((quantised, g) for g in range(PASSES))
+            else:
+                ready_passes = ()
+            for group_q, g in ready_passes:
+                h_mx_of[group_q, g] = quantise(grouped_of[group_q, g])
             done, place = group_at(step, NORM_AT)
             if done is not None and place == 0:
                 for tile_b in (0, 1):
@@ -552,11 +557,9 @@ def tile_ffnn_encoder_pa_t_kernel(
                 mean_of_squares(e, b, sums_of[group][1])
             if signalled is not None:
                 slow_signal(signalled)
-            pair, place = divmod(step, 2 * BATCH)
-            if place == 3 and 2 * pair + 3 < N_POS:
-                for stage in (to_turns, to_whole, less_whole, add_tail):
-                    for a in range(2 * pair + 3, min(2 * pair + 5, N_POS)):
-                        stage(a)
+            for stage in (to_turns, to_whole, less_whole, add_tail):
+                for a in turns_at.get(step, ()):
+                    stage(a)
             following, next_b = group_at(step + 1, 0)
             if following is not None:
                 z_of_tile = [embed_bank(next_b, half, x_t_of[following]) for half in range(HALVES)]
@@ -566,12 +569,12 @@ def tile_ffnn_encoder_pa_t_kernel(
             if ready is not None:
                 if tile_b % 2 == 0:
                     acc_v = psum_o.tile([P, 2, N_OUT], F32, bufs=1)
-                projected = (ready, tile_b, project(tile_b, h_mx_of[ready], acc_v), acc_v)
+                projected = (ready, tile_b, project(tile_b, [h_mx_of[ready, g] for g in range(PASSES)], acc_v), acc_v)
             w = regroup_weight_at.get(step)
             if w is not None:
                 w_grouped_of[w] = regroup_weight(w)
             w = quantise_weight_at.get(step)
             if w is not None:
                 quantise_weight(w, w_grouped_of[w])
-            if group is not None and b == 1 and group + 2 < N_POS:
+            if group is not None and b == 2 and group + 2 < N_POS:
                 x_t_of[group + 2] = transpose_x(group + 2)

@@ -415,35 +415,42 @@ def tile_ffnn_encoder_pa_t_kernel(
             )
             return codes, scales
 
-        def project(b, h_mx, acc_v):
+        def mx_pass(b, g, h_g, acc, first, width):
             tokens = slice(b * P, (b + 1) * P)
-            acc_qk = psum_o.tile([P, BANK], F32)
-            half_v = acc_v[:, b % 2, :]
-            for acc, first, width in ((acc_qk[:], 0, BANK), (half_v, BANK, N_OUT)):
-                for g in range(PASSES):
-                    codes, scales = h_mx[g]
-                    nc.tensor.matmul_mx(
-                        out=acc,
-                        lhsT=codes[:, tokens].bitcast(FP8X4),
-                        lhsT_scale=scales[:, tokens],
-                        rhs=w_codes[:, g, first : first + width].bitcast(FP8X4),
-                        rhs_scale=w_scales[:, g, first : first + width],
-                        start=(g == 0),
-                        stop=(g == PASSES - 1),
-                    )
+            codes, scales = h_g
+            nc.tensor.matmul_mx(
+                out=acc,
+                lhsT=codes[:, tokens].bitcast(FP8X4),
+                lhsT_scale=scales[:, tokens],
+                rhs=w_codes[:, g, first : first + width].bitcast(FP8X4),
+                rhs_scale=w_scales[:, g, first : first + width],
+                start=(g == 0),
+                stop=(g == PASSES - 1),
+            )
+
+        def project(b, h_mx, acc_v, acc_qk):
+            todo = range(PASSES) if acc_qk is None else range(1, PASSES)
+            if acc_qk is None:
+                acc_qk = psum_o.tile([P, BANK], F32)
+            for g in todo:
+                mx_pass(b, g, h_mx[g], acc_qk[:], 0, BANK)
+            for g in range(PASSES):
+                mx_pass(b, g, h_mx[g], acc_v[:, b % 2, :], BANK, N_OUT)
             return acc_qk
 
-        def add_bias(b, acc_qk, acc_v, result):
-            nc.vector.tensor_tensor(
-                out=result[:, b, 0:BANK], in0=acc_qk[:], in1=bias_qkv[:, 0:BANK], op=ALU.add
-            )
+        def add_bias(b, acc_qk, acc_v, result, group, late):
+            todo = [(group == N_POS - 1 and b in (0,), result[:, b, 0:BANK], acc_qk[:], bias_qkv[:, 0:BANK])]
             if b % 2 == 1:
-                nc.vector.tensor_tensor(
-                    out=result[:, b - 1 : b + 1, BANK:N_ALL],
-                    in0=acc_v[:],
-                    in1=bias_qkv[:, BANK:N_ALL].unsqueeze(1).to_broadcast([P, 2, N_OUT]),
-                    op=ALU.add,
-                )
+                todo.append((
+                    (group, b) in ((7, 1),),
+                    result[:, b - 1 : b + 1, BANK:N_ALL], acc_v[:],
+                    bias_qkv[:, BANK:N_ALL].unsqueeze(1).to_broadcast([P, 2, N_OUT]),
+                ))
+            for put_off, o, acc, bias in todo:
+                if put_off:
+                    late.append((o, acc, bias))
+                else:
+                    nc.vector.tensor_tensor(out=o, in0=acc, in1=bias, op=ALU.add)
 
         def store_tile(group, b, result):
             for w, out in enumerate((out_0, out_1, out_2)):
@@ -454,11 +461,11 @@ def tile_ffnn_encoder_pa_t_kernel(
                         in_=result[:, first : b + 1, w * N_OUT : (w + 1) * N_OUT],
                     )
 
-        def store_group(group, result):
+        def store_pair(group, b, result):
             for w, out in enumerate((out_0, out_1, out_2)):
                 nc.sync.dma_start(
-                    out=out.rearrange("b (a p) n -> a p b n", p=P)[group],
-                    in_=result[:, :, w * N_OUT : (w + 1) * N_OUT],
+                    out=out.rearrange("b (a p) n -> a p b n", p=P)[group][:, b - 1 : b + 1],
+                    in_=result[:, b - 1 : b + 1, w * N_OUT : (w + 1) * N_OUT],
                 )
 
         STATS_AT = 5
@@ -494,6 +501,9 @@ def tile_ffnn_encoder_pa_t_kernel(
         grouped_of = {}
         h_mx_of = {}
         w_grouped_of = {}
+        early_of = {}
+        EARLY_AT = 11
+        EARLY = 3
         projected = None
         for step in range(BATCH * N_POS + PROJECT_AT + 1):
             group, b = group_at(step, 0)
@@ -531,15 +541,19 @@ def tile_ffnn_encoder_pa_t_kernel(
             if done is not None and place == 0:
                 for tile_b in (0, 1):
                     normalise(nc.vector, tile_b, e_of[done][tile_b], *stats_of[done])
+            late = []
+            store_late = None
             if projected is not None:
                 of_group, of_b, acc_qk, acc_v_of = projected
                 if of_b == 0:
                     result = work.tile([P, BATCH, N_ALL], F32, bufs=2)
-                add_bias(of_b, acc_qk, acc_v_of, result)
-                if of_group == N_POS - 1:
+                add_bias(of_b, acc_qk, acc_v_of, result, of_group, late)
+                if late:
+                    store_late = (of_group, of_b, result)
+                elif of_group == N_POS - 1:
                     store_tile(of_group, of_b, result)
-                elif of_b == BATCH - 1:
-                    store_group(of_group, result)
+                elif of_b % 2 == 1:
+                    store_pair(of_group, of_b, result)
                 projected = None
 
             signalled = signal_at.get(step)
@@ -568,8 +582,27 @@ def tile_ffnn_encoder_pa_t_kernel(
             ready, tile_b = group_at(step, PROJECT_AT)
             if ready is not None:
                 if tile_b % 2 == 0:
-                    acc_v = psum_o.tile([P, 2, N_OUT], F32, bufs=1)
-                projected = (ready, tile_b, project(tile_b, [h_mx_of[ready, g] for g in range(PASSES)], acc_v), acc_v)
+                    if ready == N_POS - 1:
+                        acc_v = psum_z.tile([P, 2, N_OUT], F32, name="z")
+                    else:
+                        acc_v = psum_o.tile([P, 2, N_OUT], F32, bufs=1)
+                h_mx = [h_mx_of[ready, g] for g in range(PASSES)]
+                acc_qk = project(tile_b, h_mx, acc_v, early_of.get((ready, tile_b)))
+                projected = (ready, tile_b, acc_qk, acc_v)
+            if step == BATCH * (N_POS - 1) + EARLY_AT:
+                for tile_b in range(EARLY):
+                    early = psum_t.tile([P, BANK], F32, name="early", tag="tp")
+                    early_of[N_POS - 1, tile_b] = early
+                    mx_pass(tile_b, 0, h_mx_of[N_POS - 1, 0], early[:], 0, BANK)
+            for out_l, acc_l, bias_l in late:
+                nc.scalar.copy(out=out_l, in_=acc_l)
+            for out_l, acc_l, bias_l in late:
+                nc.gpsimd.tensor_tensor(out=out_l, in0=out_l, in1=bias_l, op=ALU.add)
+            if store_late is not None:
+                if store_late[0] == N_POS - 1:
+                    store_tile(*store_late)
+                elif store_late[1] % 2 == 1:
+                    store_pair(*store_late)
             w = regroup_weight_at.get(step)
             if w is not None:
                 w_grouped_of[w] = regroup_weight(w)

@@ -29,6 +29,7 @@ K_PASS = P * PACK
 PASSES = D // K_PASS
 CHUNKS = D // P
 N_POS = SEQ // P
+ROW_TILES = range(8, 16)
 GROUP = BATCH * P
 
 FLOPS = 2 * BATCH * SEQ * (FIN * D + D * N_ALL)
@@ -94,6 +95,8 @@ def tile_ffnn_encoder_pa_t_kernel(
             w_raw.append(raw)
         load_vector(1, g0)
         load_vector(2, beta0)
+        b_raw = keep.tile([P, D], BF16)
+        nc.sync.dma_start(out=b_raw[0:1, :], in_=b_emb.unsqueeze(0))
         bias_qkv = keep.tile([P, N_ALL], BF16)
         for w, vector in enumerate((bq, bk, bv)):
             nc.sync.dma_start(
@@ -126,6 +129,11 @@ def tile_ffnn_encoder_pa_t_kernel(
                 nc.scalar.mul(out=tail, in_=one[:], mul=value - head_of(value))
         warm = keep.tile([P, 1], F32)
         nc.scalar.activation(out=warm[:], in_=one[:], func=FUNC.Sin)
+        first_row = keep.tile([P, P], BF16)
+        nc.vector.memset(first_row[:], 0.0)
+        nc.vector.memset(first_row[0:1, :], 1.0)
+        b_row = keep.tile([P, D], BF16)
+        nc.vector.memset(b_row[:], 0.0)
         pos = keep.tile([P, N_POS], F32)
         nc.gpsimd.iota(
             out=pos[:], pattern=[[P, N_POS]], base=0, channel_multiplier=1,
@@ -300,17 +308,24 @@ def tile_ffnn_encoder_pa_t_kernel(
             nc.scalar.copy(out=x_t[:], in_=x_t_ps[:])
             return x_t
 
-        def embed_bank(b, half, x_t):
+        def embed_bank(tile, half, x_t):
             z = psum_z.tile([P, BANK], F32)
-            for j in range(BANK // P):
+            b = tile % BATCH
+            if tile in ROW_TILES:
                 nc.tensor.matmul(
-                    out=z[:, j * P : (j + 1) * P],
-                    lhsT=b_wide[:, half * (BANK // P) + j, :],
-                    rhs=ident_f[:],
-                    is_transpose=True,
-                    start=(j == 0),
-                    stop=False,
+                    out=z[:], lhsT=first_row[:], rhs=b_row[:, half * BANK : (half + 1) * BANK],
+                    start=True, stop=False,
                 )
+            else:
+                for j in range(BANK // P):
+                    nc.tensor.matmul(
+                        out=z[:, j * P : (j + 1) * P],
+                        lhsT=b_wide[:, half * (BANK // P) + j, :],
+                        rhs=ident_f[:],
+                        is_transpose=True,
+                        start=(j == 0),
+                        stop=False,
+                    )
             nc.tensor.matmul(
                 out=z[:],
                 lhsT=x_t[:, b * P : (b + 1) * P],
@@ -474,6 +489,7 @@ def tile_ffnn_encoder_pa_t_kernel(
         REGROUP_AT = 10
         QUANT_AT = 12
         PROJECT_AT = 13
+        ROW_AT = 1
         CHUNKS_A_STEP = CHUNKS // BATCH
 
         def group_at(step, lag):
@@ -521,7 +537,7 @@ def tile_ffnn_encoder_pa_t_kernel(
             done, place = group_at(step, STATS_AT)
             if done is not None and place == 0:
                 stats_of[done] = statistics(*sums_of[done])
-                for tile_b in (2, 3):
+                for tile_b in ((2, 3) if done < 7 else (3,)):
                     normalise(nc.gpsimd, tile_b, e_of[done][tile_b], *stats_of[done])
 
             regrouped, place = group_at(step, REGROUP_AT)
@@ -539,7 +555,7 @@ def tile_ffnn_encoder_pa_t_kernel(
                 h_mx_of[group_q, g] = quantise(grouped_of[group_q, g])
             done, place = group_at(step, NORM_AT)
             if done is not None and place == 0:
-                for tile_b in (0, 1):
+                for tile_b in ((0, 1) if done < 7 else (0, 1, 2)):
                     normalise(nc.vector, tile_b, e_of[done][tile_b], *stats_of[done])
             late = []
             store_late = None
@@ -576,7 +592,7 @@ def tile_ffnn_encoder_pa_t_kernel(
                     stage(a)
             following, next_b = group_at(step + 1, 0)
             if following is not None:
-                z_of_tile = [embed_bank(next_b, half, x_t_of[following]) for half in range(HALVES)]
+                z_of_tile = [embed_bank(step + 1, half, x_t_of[following]) for half in range(HALVES)]
             if turned is not None:
                 scale_and_shift(e_of[turned], c + 1, value_of(planes, turned, g_turned, t + 1))
             ready, tile_b = group_at(step, PROJECT_AT)
@@ -606,6 +622,10 @@ def tile_ffnn_encoder_pa_t_kernel(
             w = regroup_weight_at.get(step)
             if w is not None:
                 w_grouped_of[w] = regroup_weight(w)
+            if step == ROW_AT:
+                out_row = b_row[0:1, :].rearrange("f (g t p) -> f g t p", g=PASSES, t=PACK)
+                in_row = b_raw[0:1, :].rearrange("f (g p t) -> f g t p", g=PASSES, t=PACK)
+                nc.scalar.copy(out=out_row, in_=in_row)
             w = quantise_weight_at.get(step)
             if w is not None:
                 quantise_weight(w, w_grouped_of[w])

import math
from contextlib import ExitStack

import concourse.mybir as mybir
from concourse.masks import make_identity

F32 = mybir.dt.float32
BF16 = mybir.dt.bfloat16
I32 = mybir.dt.int32
U32 = mybir.dt.uint32
U8 = mybir.dt.uint8
FP8X4 = mybir.dt.float8_e4m3fn_x4
ALU = mybir.AluOpType
FUNC = mybir.ActivationFunctionType

P = 128
BATCH = 4
SEQ = 1024
FIN = 128
D = 1024
ROOT_D = 32
N_OUT = 256
N_ALL = 3 * N_OUT
EPS = 1e-3
BANK = 512
HALVES = D // BANK
PACK = 4
K_PASS = P * PACK
PASSES = D // K_PASS
CHUNKS = D // P
N_POS = SEQ // P
ROW_TILES = range(8, 16)
GROUP = BATCH * P

FLOPS = 2 * BATCH * SEQ * (FIN * D + D * N_ALL)

N_FREQ = D // 2
LOG_STEP = math.log(10000.0) / (N_FREQ - 1)
FINE = 32
COARSE = N_FREQ // FINE
QUADS = FINE // PACK
HEAD_BITS = 12
ROUND_TO_INT = 12582912.0


def head_of(value):
    exponent = math.floor(math.log(value) / math.log(2.0))
    step = 2.0 ** (exponent - HEAD_BITS + 1)
    return round(value / step) * step


def fast_quads(a):
    last = P * a + P - 1
    return math.ceil(math.log(last / math.pi) / LOG_STEP / PACK)


FAST_COARSE = math.ceil(fast_quads(N_POS - 1) / QUADS)
SLOW_FROM = fast_quads(0) // QUADS


def tile_ffnn_encoder_pa_t_kernel(
    tc, x, W_emb, b_emb, g0, beta0, Wq, bq, Wk, bk, Wv, bv, out_0, out_1, out_2
):
    nc = tc.nc
    with ExitStack() as ctx:
        ctx.enter_context(tc.manual_schedule())
        keep = ctx.enter_context(tc.tile_pool(name="keep", bufs=1))
        work = ctx.enter_context(tc.tile_pool(name="work", bufs=2))
        psum_z = ctx.enter_context(tc.psum_pool(name="psum_z", bufs=2))
        psum_t = ctx.enter_context(tc.psum_pool(name="psum_t", bufs=3))
        psum_o = ctx.enter_context(tc.psum_pool(name="psum_o", bufs=2))

        x_by_pos = x.rearrange("b (a p) f -> a p b f", p=P)
        x_sb = keep.tile([P, N_POS, BATCH, FIN], BF16)
        nc.sync.dma_start(out=x_sb[:, 0], in_=x_by_pos[0])
        vectors = keep.tile([P, 3, 2 * CHUNKS], BF16)

        def load_vector(v, vector):
            nc.sync.dma_start(
                out=vectors[:, v, 0:CHUNKS].rearrange("p (g t) -> p g t", t=PACK),
                in_=vector.rearrange("(g p t) -> p g t", p=P, t=PACK),
            )

        load_vector(0, b_emb)
        w_emb_raw = keep.tile([P, D], BF16)
        nc.sync.dma_start(out=w_emb_raw[:], in_=W_emb)
        for a in range(1, N_POS):
            nc.sync.dma_start(out=x_sb[:, a], in_=x_by_pos[a])
        w_raw = []
        for w, weight in enumerate((Wq, Wk, Wv)):
            raw = keep.tile([P, PASSES, PACK, N_OUT], BF16, name="w_raw%d" % w)
            nc.sync.dma_start(
                out=raw[:], in_=weight.rearrange("(g p t) n -> p g t n", p=P, t=PACK)
            )
            w_raw.append(raw)
        load_vector(1, g0)
        load_vector(2, beta0)
        b_raw = keep.tile([P, D], BF16)
        nc.sync.dma_start(out=b_raw[0:1, :], in_=b_emb.unsqueeze(0))
        bias_qkv = keep.tile([P, N_ALL], BF16)
        for w, vector in enumerate((bq, bk, bv)):
            nc.sync.dma_start(
                out=bias_qkv[:, w * N_OUT : (w + 1) * N_OUT], in_=vector.partition_broadcast(P)
            )

        one = keep.tile([P, 1], F32)
        nc.vector.memset(one[:], 1.0)
        quarter_turn = keep.tile([P, 1], F32)
        nc.scalar.mul(out=quarter_turn[:], in_=one[:], mul=0.5 * math.pi)
        ident_b = keep.tile([P, P], BF16)
        make_identity(nc, ident_b[:])
        coarse_hd = keep.tile([P, COARSE], F32)
        coarse_tl = keep.tile([P, COARSE], F32)
        fine_hd = keep.tile([P, FINE], F32)
        fine_tl = keep.tile([P, FINE], F32)
        coarse_values = [math.exp(-FINE * i * LOG_STEP) / (2.0 * math.pi) for i in range(COARSE)]
        fine_values = [math.exp(-i * LOG_STEP) for i in range(FINE)]
        for i, value in enumerate(coarse_values):
            nc.vector.memset(coarse_hd[:, i : i + 1], head_of(value))
            nc.scalar.mul(out=coarse_tl[:, i : i + 1], in_=one[:], mul=value - head_of(value))
        for i, value in enumerate(fine_values):
            head = fine_hd[:, i : i + 1]
            tail = fine_tl[:, i : i + 1]
            if i < FINE // 2:
                nc.vector.memset(head, head_of(value))
                nc.vector.tensor_scalar_mul(tail, one[:], value - head_of(value))
            else:
                nc.gpsimd.memset(head, head_of(value))
                nc.scalar.mul(out=tail, in_=one[:], mul=value - head_of(value))
        warm = keep.tile([P, 1], F32)
        nc.scalar.activation(out=warm[:], in_=one[:], func=FUNC.Sin)
        first_row = keep.tile([P, P], BF16)
        nc.vector.memset(first_row[:], 0.0)
        nc.vector.memset(first_row[0:1, :], 1.0)
        b_row = keep.tile([P, D], BF16)
        nc.vector.memset(b_row[:], 0.0)
        pos = keep.tile([P, N_POS], F32)
        nc.gpsimd.iota(
            out=pos[:], pattern=[[P, N_POS]], base=0, channel_multiplier=1,
            allow_small_or_imprecise_dtypes=True,
        )
        angle = keep.tile([P, N_POS], F32)
        nc.gpsimd.tensor_scalar(
            out=angle[:], in0=pos[:], scalar1=2.0 * math.pi, scalar2=0.0, op0=ALU.mult, op1=ALU.add
        )
        minus_angle = keep.tile([P, N_POS], F32)
        nc.gpsimd.tensor_scalar(
            out=minus_angle[:], in0=pos[:], scalar1=-2.0 * math.pi, scalar2=0.0, op0=ALU.mult, op1=ALU.add
        )
        minus_eighth = keep.tile([P, 1], F32)
        nc.gpsimd.memset(minus_eighth[:], -0.125)
        plus_eighth = keep.tile([P, 1], F32)
        nc.gpsimd.memset(plus_eighth[:], 0.125)
        ident_f = keep.tile([P, P], F32)
        make_identity(nc, ident_f[:])
        b_wide = keep.tile([P, CHUNKS, P], F32)
        nc.gpsimd.tensor_scalar(
            out=b_wide[:], in0=vectors[:, 0, 0:CHUNKS].unsqueeze(2).to_broadcast([P, CHUNKS, P]),
            scalar1=1.0, scalar2=0.0, op0=ALU.mult, op1=ALU.add,
        )
        minus_half = keep.tile([P, BATCH], F32)
        nc.gpsimd.memset(minus_half[:], -0.5)

        def over_fine(table, first, last):
            cells = table[:, first:last].unsqueeze(2).unsqueeze(3)
            return cells.to_broadcast([P, last - first, QUADS, PACK])

        def over_coarse(table, count):
            quads = table[:].rearrange("p (q t) -> p q t", t=PACK)
            return quads.unsqueeze(1).to_broadcast([P, count, QUADS, PACK])

        def as_grid(table):
            return table[:].rearrange("p t (a q) -> p a q t", q=QUADS)

        fast_shape = [P, PACK, FAST_COARSE * QUADS]
        product = keep.tile(fast_shape, F32)
        cross = keep.tile(fast_shape, F32)
        cross2 = keep.tile(fast_shape, F32)
        f_head = keep.tile(fast_shape, F32)
        f_tail = keep.tile(fast_shape, F32)
        f_slow = keep.tile([P, PACK, (COARSE - SLOW_FROM) * QUADS], F32)
        fine_all = keep.tile([P, FINE], F32)
        coarse_all = keep.tile([P, COARSE], F32)
        turns_of = {}
        whole_of = {}
        frac_of = {}

        def to_turns(a):
            turns_of[a] = work.tile([P, PACK, fast_quads(a)], F32, name="turns", bufs=3)
            nc.vector.tensor_scalar(
                out=turns_of[a][:], in0=f_head[:, :, 0 : fast_quads(a)],
                scalar1=pos[:, a : a + 1], scalar2=-0.125, op0=ALU.mult, op1=ALU.add,
            )

        def to_whole(a):
            whole_of[a] = work.tile([P, PACK, fast_quads(a)], F32, name="whole", bufs=3)
            nc.vector.tensor_scalar(
                out=whole_of[a][:], in0=turns_of[a][:], scalar1=ROUND_TO_INT,
                scalar2=ROUND_TO_INT, op0=ALU.add, op1=ALU.subtract,
            )

        def less_whole(a):
            nc.vector.tensor_tensor(
                out=whole_of[a][:], in0=turns_of[a][:], in1=whole_of[a][:], op=ALU.subtract
            )

        def add_tail(a):
            frac_of[a] = work.tile([P, PACK, fast_quads(a)], F32, name="frac", bufs=5)
            nc.vector.scalar_tensor_tensor(
                out=frac_of[a][:], in0=f_tail[:, :, 0 : fast_quads(a)],
                scalar=pos[:, a : a + 1], in1=whole_of[a][:], op0=ALU.mult, op1=ALU.add,
            )

        nc.vector.tensor_tensor(
            out=as_grid(product), in0=over_fine(coarse_hd, 0, FAST_COARSE),
            in1=over_coarse(fine_hd, FAST_COARSE), op=ALU.mult,
        )
        nc.vector.tensor_tensor(out=coarse_all[:], in0=coarse_hd[:], in1=coarse_tl[:], op=ALU.add)
        nc.vector.tensor_single_scalar(
            out=f_head[:].bitcast(I32), in_=product[:].bitcast(I32), scalar=-2048, op=ALU.bitwise_and
        )
        nc.vector.tensor_tensor(out=fine_all[:], in0=fine_hd[:], in1=fine_tl[:], op=ALU.add)
        nc.vector.tensor_tensor(
            out=as_grid(cross), in0=over_fine(coarse_hd, 0, FAST_COARSE),
            in1=over_coarse(fine_tl, FAST_COARSE), op=ALU.mult,
        )
        to_turns(0)
        nc.vector.tensor_tensor(out=product[:], in0=product[:], in1=f_head[:], op=ALU.subtract)
        nc.vector.tensor_tensor(
            out=as_grid(f_slow), in0=over_fine(coarse_all, SLOW_FROM, COARSE),
            in1=over_coarse(fine_all, COARSE - SLOW_FROM), op=ALU.mult,
        )
        to_whole(0)
        nc.vector.tensor_tensor(out=cross[:], in0=product[:], in1=cross[:], op=ALU.add)
        nc.vector.tensor_tensor(
            out=as_grid(cross2), in0=over_fine(coarse_tl, 0, FAST_COARSE),
            in1=over_coarse(fine_all, FAST_COARSE), op=ALU.mult,
        )
        less_whole(0)
        nc.vector.tensor_tensor(out=f_tail[:], in0=cross[:], in1=cross2[:], op=ALU.add)
        to_turns(1)
        to_turns(2)
        add_tail(0)
        for stage in (to_whole, less_whole, add_tail):
            for a in (1, 2):
                stage(a)

        w_emb = keep.tile([P, D], BF16)
        for g in range(PASSES):
            span = slice(g * K_PASS, (g + 1) * K_PASS)
            nc.scalar.copy(
                out=w_emb[:, span].rearrange("f (t p) -> f t p", t=PACK),
                in_=w_emb_raw[:, span].rearrange("f (p t) -> f t p", t=PACK),
            )

        w_codes = keep.tile([P, PASSES, N_ALL], U32, align_bytes=64)
        w_scales = keep.tile([P, PASSES, N_ALL], U8, align_bytes=64)

        def regroup_weight(w):
            w_grouped = work.tile([P, PASSES, N_OUT, PACK], BF16, bufs=3, align_bytes=64)
            src = w_raw[w][:].rearrange("p g t n -> p g n t")
            nc.gpsimd.tensor_scalar(
                out=w_grouped[:], in0=src, scalar1=1.0, scalar2=0.0, op0=ALU.mult, op1=ALU.add
            )
            return w_grouped

        def quantise_weight(w, w_grouped):
            for g in range(PASSES):
                cols_w = slice(w * N_OUT, (w + 1) * N_OUT)
                nc.vector.quantize_mx(
                    out=w_codes[:, g, cols_w].bitcast(FP8X4),
                    scales=w_scales[:, g, cols_w],
                    in_=w_grouped[:, g].rearrange("p n t -> p (n t)"),
                )

        timing = keep.tile([P, N_POS, 2, PACK, P], F32)

        def fast_signal(a, frac):
            fast = fast_quads(a)
            for half, shift in enumerate((minus_eighth, plus_eighth)):
                distance = work.tile([P, PACK, fast], F32, bufs=3)
                nc.scalar.activation(
                    out=distance[:], in_=frac[:], func=FUNC.Abs, bias=shift[:], scale=1.0
                )
                nc.scalar.activation(
                    out=timing[:, a, half, :, 0:fast], in_=distance[:], func=FUNC.Sin,
                    bias=quarter_turn[:], scale=-2.0 * math.pi,
                )

        def slow_signal(a):
            fast = fast_quads(a)
            f_here = f_slow[:, :, fast - SLOW_FROM * QUADS :]
            nc.scalar.activation(
                out=timing[:, a, 0, :, fast:P], in_=f_here, func=FUNC.Sin, scale=angle[:, a : a + 1]
            )
            nc.scalar.activation(
                out=timing[:, a, 1, :, fast:P], in_=f_here, func=FUNC.Sin,
                bias=quarter_turn[:], scale=minus_angle[:, a : a + 1],
            )

        def transpose_x(a):
            x_t_ps = psum_t.tile([P, GROUP], BF16, tag="tp")
            for b in range(BATCH):
                nc.tensor.transpose(
                    out=x_t_ps[:, b * P : (b + 1) * P], in_=x_sb[:, a, b, :], identity=ident_b[:]
                )
            x_t = work.tile([P, GROUP], BF16, bufs=3)
            nc.scalar.copy(out=x_t[:], in_=x_t_ps[:])
            return x_t

        def embed_bank(tile, half, x_t):
            z = psum_z.tile([P, BANK], F32)
            b = tile % BATCH
            if tile in ROW_TILES:
                nc.tensor.matmul(
                    out=z[:], lhsT=first_row[:], rhs=b_row[:, half * BANK : (half + 1) * BANK],
                    start=True, stop=False,
                )
            else:
                for j in range(BANK // P):
                    nc.tensor.matmul(
                        out=z[:, j * P : (j + 1) * P],
                        lhsT=b_wide[:, half * (BANK // P) + j, :],
                        rhs=ident_f[:],
                        is_transpose=True,
                        start=(j == 0),
                        stop=False,
                    )
            nc.tensor.matmul(
                out=z[:],
                lhsT=x_t[:, b * P : (b + 1) * P],
                rhs=w_emb[:, half * BANK : (half + 1) * BANK],
                start=False,
                stop=True,
            )
            return z

        def add_timing(a, b, half, z, e, sum_e):
            nc.vector.scalar_tensor_tensor(
                out=e[:, half * BANK : (half + 1) * BANK],
                in0=z[:],
                scalar=0.0,
                in1=timing[:, a, half].rearrange("p t q -> p (t q)"),
                op0=ALU.max,
                op1=ALU.add,
                accum_out=sum_e[:, b, half : half + 1],
            )

        def mean_of_squares(e, b, mean_sq):
            squares = work.tile([P, D], BF16, bufs=2)
            nc.scalar.activation(
                out=squares[:], in_=e[:], func=FUNC.Square, scale=1.0 / ROOT_D,
                accum_out=mean_sq[:, b : b + 1],
            )

        def statistics(sum_e, mean_sq):
            total = work.tile([P, BATCH], F32, bufs=2)
            nc.gpsimd.tensor_tensor(out=total[:], in0=sum_e[:, :, 0], in1=sum_e[:, :, 1], op=ALU.add)
            minus_mean = work.tile([P, BATCH], F32, bufs=2)
            nc.gpsimd.tensor_scalar(
                out=minus_mean[:], in0=total[:], scalar1=-1.0 / D, scalar2=0.0, op0=ALU.mult, op1=ALU.add
            )
            less_eps = work.tile([P, BATCH], F32, bufs=2)
            nc.gpsimd.tensor_tensor(out=less_eps[:], in0=minus_mean[:], in1=minus_mean[:], op=ALU.mult)
            nc.gpsimd.tensor_scalar(
                out=less_eps[:], in0=less_eps[:], scalar1=1.0, scalar2=-EPS, op0=ALU.mult, op1=ALU.add
            )
            var_eps = work.tile([P, BATCH], F32, bufs=2)
            nc.gpsimd.tensor_tensor(out=var_eps[:], in0=mean_sq[:], in1=less_eps[:], op=ALU.subtract)
            rstd = work.tile([P, BATCH], F32, bufs=2)
            nc.gpsimd.tensor_tensor(out=rstd[:], in0=var_eps[:], in1=minus_half[:], op=ALU.pow)
            return minus_mean, rstd

        def normalise(engine, b, e, minus_mean, rstd):
            width = D // 2 if engine is nc.gpsimd else D
            for first in range(0, D, width):
                part = e[:, first : first + width]
                engine.tensor_scalar(
                    out=part, in0=part, scalar1=minus_mean[:, b : b + 1],
                    scalar2=rstd[:, b : b + 1], op0=ALU.add, op1=ALU.mult,
                )

        def scale_and_shift(normed_tiles, c, half):
            normed_t = psum_t.tile([P, GROUP], F32, tag="tp")
            for b in range(BATCH):
                nc.tensor.transpose(
                    out=normed_t[:, b * P : (b + 1) * P],
                    in_=normed_tiles[b][:, c * P : (c + 1) * P],
                    identity=ident_f[:],
                )
            nc.scalar.activation(
                out=half, in_=normed_t[:], func=FUNC.Identity,
                scale=cols[:, CHUNKS + c : CHUNKS + c + 1],
                bias=cols[:, 2 * CHUNKS + c : 2 * CHUNKS + c + 1],
            )

        def is_paired(group, g):
            return not (g == 1)

        def new_planes(group, g):
            shape = [P, PACK // 2, GROUP, 2] if is_paired(group, g) else [P, PACK, GROUP]
            return work.tile(shape, BF16, name="planes", tag="planes", bufs=4)

        def value_of(planes, group, g, t):
            return planes[:, t // 2, :, t % 2] if is_paired(group, g) else planes[:, t, :]

        def regroup(planes, group, g):
            grouped = work.tile([P, GROUP, PACK], BF16, bufs=2, align_bytes=64)
            if is_paired(group, g):
                nc.vector.tensor_copy(
                    out=grouped[:].rearrange("p r t -> p (r t)").bitcast(F32)
                    .rearrange("p (r u) -> p r u", u=PACK // 2),
                    in_=planes[:].rearrange("p u r e -> p (u r e)").bitcast(F32)
                    .rearrange("p (u r) -> p r u", u=PACK // 2),
                )
            else:
                nc.vector.tensor_copy(
                    out=grouped[:].rearrange("p (k i) t -> p k t i", i=4),
                    in_=planes[:].rearrange("p t (k i) -> p k t i", i=4),
                )
            return grouped

        def quantise(grouped):
            codes = work.tile([P, GROUP], U32, bufs=4, align_bytes=64)
            scales = work.tile([P, GROUP], U8, bufs=4, align_bytes=64)
            nc.vector.quantize_mx(
                out=codes[:].bitcast(FP8X4),
                scales=scales[:],
                in_=grouped[:].rearrange("p r t -> p (r t)"),
            )
            return codes, scales

        def mx_pass(b, g, h_g, acc, first, width):
            tokens = slice(b * P, (b + 1) * P)
            codes, scales = h_g
            nc.tensor.matmul_mx(
                out=acc,
                lhsT=codes[:, tokens].bitcast(FP8X4),
                lhsT_scale=scales[:, tokens],
                rhs=w_codes[:, g, first : first + width].bitcast(FP8X4),
                rhs_scale=w_scales[:, g, first : first + width],
                start=(g == 0),
                stop=(g == PASSES - 1),
            )

        def project(b, h_mx, acc_v, acc_qk):
            todo = range(PASSES) if acc_qk is None else range(1, PASSES)
            if acc_qk is None:
                acc_qk = psum_o.tile([P, BANK], F32)
            for g in todo:
                mx_pass(b, g, h_mx[g], acc_qk[:], 0, BANK)
            for g in range(PASSES):
                mx_pass(b, g, h_mx[g], acc_v[:, b % 2, :], BANK, N_OUT)
            return acc_qk

        def add_bias(b, acc_qk, acc_v, result, group, late):
            todo = [(group == N_POS - 1 and b in (0,), result[:, b, 0:BANK], acc_qk[:], bias_qkv[:, 0:BANK])]
            if b % 2 == 1:
                todo.append((
                    (group, b) in ((7, 1),),
                    result[:, b - 1 : b + 1, BANK:N_ALL], acc_v[:],
                    bias_qkv[:, BANK:N_ALL].unsqueeze(1).to_broadcast([P, 2, N_OUT]),
                ))
            for put_off, o, acc, bias in todo:
                if put_off:
                    late.append((o, acc, bias))
                else:
                    nc.vector.tensor_tensor(out=o, in0=acc, in1=bias, op=ALU.add)

        def store_tile(group, b, result):
            for w, out in enumerate((out_0, out_1, out_2)):
                first = b if w < 2 else b - 1
                if w < 2 or b % 2 == 1:
                    nc.sync.dma_start(
                        out=out.rearrange("b (a p) n -> a p b n", p=P)[group][:, first : b + 1],
                        in_=result[:, first : b + 1, w * N_OUT : (w + 1) * N_OUT],
                    )

        def store_pair(group, b, result):
            for w, out in enumerate((out_0, out_1, out_2)):
                nc.sync.dma_start(
                    out=out.rearrange("b (a p) n -> a p b n", p=P)[group][:, b - 1 : b + 1],
                    in_=result[:, b - 1 : b + 1, w * N_OUT : (w + 1) * N_OUT],
                )

        STATS_AT = 5
        NORM_AT = 6
        TURN_AT = 7
        REGROUP_AT = 10
        QUANT_AT = 12
        PROJECT_AT = 13
        ROW_AT = 1
        CHUNKS_A_STEP = CHUNKS // BATCH

        def group_at(step, lag):
            group, place = divmod(step - lag, BATCH)
            return (group if 0 <= group < N_POS else None), place

        signal_at = {(3 * (a - 1) if a < 4 else BATCH * a - 2): a for a in range(1, N_POS)}
        turns_at = {4: (3, 4), 11: (5, 6), 19: (7,)}
        regroup_weight_at = {1 + w: w for w in range(3)}
        quantise_weight_at = {7 + w: w for w in range(3)}

        cols = keep.tile([P, 3 * CHUNKS], F32)
        x_t_of = {0: transpose_x(0)}
        z_of_tile = [embed_bank(0, half, x_t_of[0]) for half in range(HALVES)]
        slow_signal(0)
        fast_signal(0, frac_of[0])
        x_t_of[1] = transpose_x(1)
        nc.gpsimd.tensor_copy(
            out=cols[:].rearrange("p (v c) -> p v c", v=3), in_=vectors[:, :, 0:CHUNKS]
        )
        sums_of = {}
        e_of = {}
        stats_of = {}
        planes_of = {}
        grouped_of = {}
        h_mx_of = {}
        w_grouped_of = {}
        early_of = {}
        EARLY_AT = 11
        EARLY = 3
        projected = None
        for step in range(BATCH * N_POS + PROJECT_AT + 1):
            group, b = group_at(step, 0)
            if group is not None:
                if b == 0:
                    sum_e = work.tile([P, BATCH, HALVES], F32, bufs=3)
                    mean_sq = work.tile([P, BATCH], F32, bufs=3)
                    sums_of[group] = (sum_e, mean_sq)
                    e_of[group] = []
                e = work.tile([P, D], F32, bufs=14)
                e_of[group].append(e)
                for half in range(HALVES):
                    add_timing(group, b, half, z_of_tile[half], e, sums_of[group][0])

            done, place = group_at(step, STATS_AT)
            if done is not None and place == 0:
                stats_of[done] = statistics(*sums_of[done])
                for tile_b in ((2, 3) if done < 7 else (3,)):
                    normalise(nc.gpsimd, tile_b, e_of[done][tile_b], *stats_of[done])

            regrouped, place = group_at(step, REGROUP_AT)
            g, odd = divmod(place, 2)
            if regrouped is not None and odd == 0:
                grouped_of[regrouped, g] = regroup(planes_of[regrouped, g], regrouped, g)
            quantised, place = group_at(step, QUANT_AT)
            if regrouped == N_POS - 1 and odd == 0:
                ready_passes = ((regrouped, g),)
            elif quantised is not None and quantised < N_POS - 1 and place == 0:
                ready_passes = tuple((quantised, g) for g in range(PASSES))
            else:
                ready_passes = ()
            for group_q, g in ready_passes:
                h_mx_of[group_q, g] = quantise(grouped_of[group_q, g])
            done, place = group_at(step, NORM_AT)
            if done is not None and place == 0:
                for tile_b in ((0, 1) if done < 7 else (0, 1, 2)):
                    normalise(nc.vector, tile_b, e_of[done][tile_b], *stats_of[done])
            late = []
            store_late = None
            if projected is not None:
                of_group, of_b, acc_qk, acc_v_of = projected
                if of_b == 0:
                    result = work.tile([P, BATCH, N_ALL], F32, bufs=2)
                add_bias(of_b, acc_qk, acc_v_of, result, of_group, late)
                if late:
                    store_late = (of_group, of_b, result)
                elif of_group == N_POS - 1:
                    store_tile(of_group, of_b, result)
                elif of_b % 2 == 1:
                    store_pair(of_group, of_b, result)
                projected = None

            signalled = signal_at.get(step)
            if signalled is not None:
                fast_signal(signalled, frac_of[signalled])
            turned, j = group_at(step, TURN_AT)
            c = j * CHUNKS_A_STEP
            if turned is not None:
                g_turned, t = divmod(c, PACK)
                if t == 0:
                    planes_of[turned, g_turned] = new_planes(turned, g_turned)
                planes = planes_of[turned, g_turned]
                scale_and_shift(e_of[turned], c, value_of(planes, turned, g_turned, t))
            if group is not None:
                mean_of_squares(e, b, sums_of[group][1])
            if signalled is not None:
                slow_signal(signalled)
            for stage in (to_turns, to_whole, less_whole, add_tail):
                for a in turns_at.get(step, ()):
                    stage(a)
            following, next_b = group_at(step + 1, 0)
            if following is not None:
                z_of_tile = [embed_bank(step + 1, half, x_t_of[following]) for half in range(HALVES)]
            if turned is not None:
                scale_and_shift(e_of[turned], c + 1, value_of(planes, turned, g_turned, t + 1))
            ready, tile_b = group_at(step, PROJECT_AT)
            if ready is not None:
                if tile_b % 2 == 0:
                    if ready == N_POS - 1:
                        acc_v = psum_z.tile([P, 2, N_OUT], F32, name="z")
                    else:
                        acc_v = psum_o.tile([P, 2, N_OUT], F32, bufs=1)
                h_mx = [h_mx_of[ready, g] for g in range(PASSES)]
                acc_qk = project(tile_b, h_mx, acc_v, early_of.get((ready, tile_b)))
                projected = (ready, tile_b, acc_qk, acc_v)
            if step == BATCH * (N_POS - 1) + EARLY_AT:
                for tile_b in range(EARLY):
                    early = psum_t.tile([P, BANK], F32, name="early", tag="tp")
                    early_of[N_POS - 1, tile_b] = early
                    mx_pass(tile_b, 0, h_mx_of[N_POS - 1, 0], early[:], 0, BANK)
            for out_l, acc_l, bias_l in late:
                nc.scalar.copy(out=out_l, in_=acc_l)
            for out_l, acc_l, bias_l in late:
                nc.gpsimd.tensor_tensor(out=out_l, in0=out_l, in1=bias_l, op=ALU.add)
            if store_late is not None:
                if store_late[0] == N_POS - 1:
                    store_tile(*store_late)
                elif store_late[1] % 2 == 1:
                    store_pair(*store_late)
            w = regroup_weight_at.get(step)
            if w is not None:
                w_grouped_of[w] = regroup_weight(w)
            if step == ROW_AT:
                out_row = b_row[0:1, :].rearrange("f (g t p) -> f g t p", g=PASSES, t=PACK)
                in_row = b_raw[0:1, :].rearrange("f (g p t) -> f g t p", g=PASSES, t=PACK)
                nc.scalar.copy(out=out_row, in_=in_row)
            w = quantise_weight_at.get(step)
            if w is not None:
                quantise_weight(w, w_grouped_of[w])
            if group is not None and b == 2 and group + 2 < N_POS:
                x_t_of[group + 2] = transpose_x(group + 2)
